import numpy as np
import ml_dtypes


def mxq(x, axis, fmt="e4m3"):
    dtype, down = {"e4m3": (ml_dtypes.float8_e4m3fn, 7), "e5m2": (ml_dtypes.float8_e5m2, 14)}[fmt]
    v = np.moveaxis(np.asarray(x, np.float32).astype(ml_dtypes.bfloat16).astype(np.float64), axis, -1)
    blocks = v.reshape(v.shape[:-1] + (-1, 32))
    amax = np.abs(blocks).max(-1, keepdims=True)
    byte = np.maximum(np.where(amax > 0, np.frexp(amax)[1] - 1 + 127, 0) - down, 1)
    scale = np.exp2(byte - 127.0)
    codes = (blocks / scale).astype(np.float32).astype(dtype).astype(np.float64)
    return np.moveaxis((codes * scale).reshape(v.shape), -1, axis)


WIDE = False


def mx_kscale(k):
    if not WIDE:
        return np.ones(k)
    levels = np.array([10, -10, 5, -5, 0])
    if k % 512:
        return np.exp2(np.random.permutation(np.resize(levels, k // 32))).repeat(32)
    a = np.empty((k // 512, 16))
    for p in range(k // 512):
        a[p, :8] = np.random.permutation(np.resize(levels, 8))
        for g in range(8):
            far = levels[np.abs(levels - a[p, g]) >= 10]
            a[p, g + 8] = far[np.random.randint(len(far))]
    return np.exp2(a.ravel()).repeat(32)


BF16 = ml_dtypes.bfloat16


def bf(x):
    return np.asarray(x, np.float32).astype(BF16)


def f64(x):
    return np.asarray(x).astype(np.float64)


B, M, K, N = 4, 1024, 1024, 1024
THRESHOLD = 1e-6
TILE = 64
LIVE = 4e-6
QUIET = 8e-7


def mask_inactive_tiles(a, threshold, tile=TILE):
    nb, m, k = a.shape
    blocks = np.abs(a).reshape(nb, m // tile, tile, k // tile, tile)
    active = blocks.max(axis=(2, 4)) > threshold
    mask = np.repeat(np.repeat(active, tile, axis=1), tile, axis=2)
    return a * mask.astype(a.dtype)


def setup_inputs():
    s = mx_kscale(K)
    lv = LIVE / s.min()
    live = np.random.random((B, M // TILE, K // TILE)) < 0.75
    livem = np.repeat(np.repeat(live, TILE, axis=1), TILE, axis=2)
    a_live = np.random.standard_normal((B, M, K)) * lv * s
    a_quiet = np.random.uniform(-QUIET, QUIET, (B, M, K))
    return {"a": bf(np.where(livem, a_live, a_quiet)),
            "b": bf(np.random.standard_normal((B, K, N)) / np.sqrt(K) / lv / s[:, None])}


def reference(a, b):
    a_sp = mask_inactive_tiles(f64(a), THRESHOLD)
    return mxq(a_sp, 2, "e4m3") @ mxq(f64(b), 1, "e4m3")

@@ -1,0 +1,240 @@
+from contextlib import ExitStack
+
+import concourse.mybir as mybir
+from concourse.masks import make_identity
+
+FLOPS = 2 * 4 * 1024 * 1024 * 1024
+
+BF16 = mybir.dt.bfloat16
+F32 = mybir.dt.float32
+I32 = mybir.dt.int32
+U32 = mybir.dt.uint32
+U8 = mybir.dt.uint8
+FP8X4 = mybir.dt.float8_e4m3fn_x4
+ALU = mybir.AluOpType
+AX = mybir.AxisListType
+
+P = 128
+NB = 4
+THRESHOLD = 1e-6
+PIN = False
+G_COLS = 256
+
+
+def tile_sparsebmm_t_kernel(tc, a, b, out):
+    nc = tc.nc
+    with ExitStack() as ctx:
+        const = ctx.enter_context(tc.tile_pool(name="const", bufs=1))
+        raw = ctx.enter_context(tc.tile_pool(name="raw", bufs=3))
+        scr = ctx.enter_context(tc.tile_pool(name="scr", bufs=1))
+        small = ctx.enter_context(tc.tile_pool(name="small", bufs=2))
+        gap = ctx.enter_context(tc.tile_pool(name="gap", bufs=4))
+        gbp = ctx.enter_context(tc.tile_pool(name="gbp", bufs=4))
+        codes = ctx.enter_context(tc.tile_pool(name="codes", bufs=2))
+        outp = ctx.enter_context(tc.tile_pool(name="outp", bufs=3))
+        ps_xt = ctx.enter_context(tc.psum_pool(name="ps_xt", bufs=3))
+        ps_acc = ctx.enter_context(tc.psum_pool(name="ps_acc", bufs=4))
+        ps_cnt = ctx.enter_context(tc.psum_pool(name="ps_cnt", bufs=1))
+        if PIN:
+            ctx.enter_context(tc.manual_schedule())
+
+        a_raw = []
+        b_raw = []
+        for i in range(NB):
+            a_t = raw.tile([P, 8192], BF16, tag="a_raw", name="a_raw%d" % i)
+            b_t = raw.tile([P, 8192], BF16, tag="b_raw", name="b_raw%d" % i)
+            a_raw.append(a_t)
+            b_raw.append(b_t)
+            a_view = a[i].rearrange("(p j) k -> p (j k)", j=8)
+            for c in range(2):
+                nc.sync.dma_start(out=a_t[:, 4096 * c:4096 * (c + 1)], in_=a_view[:, 4096 * c:4096 * (c + 1)])
+            for g in range(2):
+                nc.sync.dma_start(
+                    out=b_t[:, 4096 * g:4096 * (g + 1)],
+                    in_=b[i][512 * g:512 * (g + 1), :].rearrange("(q t) n -> q (t n)", t=4),
+                )
+
+        ident = const.tile([P, P], F32)
+        make_identity(nc, ident[:])
+        blk = const.tile([P, 16], F32)
+        nc.vector.tensor_reduce(out=blk[:], in_=ident[:].rearrange("p (g c) -> p g c", c=8), axis=AX.X, op=ALU.add)
+        group_ones = const.tile([P, P], BF16)
+        nc.vector.tensor_copy(
+            out=group_ones[:].rearrange("p (g c) -> p g c", c=8),
+            in_=blk[:].unsqueeze(2).to_broadcast([P, 16, 8]),
+        )
+        ind = const.tile([P, 32 * NB], BF16)
+        nc.vector.memset(ind[:].bitcast(I32), 0)
+
+        state = {}
+
+        def absmax(i, c):
+            ab = scr.tile([P, 4096], BF16, tag="ab", name="ab_%d_%d" % (i, c))
+            nc.vector.tensor_scalar(
+                out=ab[:].bitcast(I32),
+                in0=a_raw[i][:, 4096 * c:4096 * (c + 1)].bitcast(I32),
+                scalar1=0x7FFF7FFF, scalar2=None, op0=ALU.bitwise_and,
+            )
+            nc.vector.tensor_tensor(out=ab[:, 0:2048], in0=ab[:, 0:2048], in1=ab[:, 2048:4096], op=ALU.max)
+            hm = scr.tile([P, 1024], BF16, tag="hm%d" % c, name="hm_%d_%d" % (i, c))
+            state["hm", i, c] = hm
+            nc.vector.tensor_tensor(out=hm[:], in0=ab[:, 0:1024], in1=ab[:, 1024:2048], op=ALU.max)
+
+        def chain_a(i):
+            h0 = state["hm", i, 0]
+            nc.vector.tensor_tensor(out=h0[:], in0=h0[:], in1=state["hm", i, 1][:], op=ALU.max)
+            rm = small.tile([P, 16], F32, tag="rm", name="rm_%d" % i)
+            nc.vector.tensor_reduce(out=rm[:], in_=h0[:].rearrange("p (t k) -> p t k", k=64), axis=AX.X, op=ALU.max)
+            nc.vector.tensor_scalar(
+                out=ind[:, 32 * i:32 * i + 16], in0=rm[:], scalar1=THRESHOLD, scalar2=None, op0=ALU.is_gt
+            )
+
+        def count(i):
+            cnt = ps_cnt.tile([P, 32], F32, tag="cnt", name="cnt_%d" % i)
+            state["cnt", i] = cnt
+            nc.tensor.matmul(out=cnt[:], lhsT=group_ones[:], rhs=ind[:, 32 * i:32 * (i + 1)], start=True, stop=True)
+
+        def chain_b(i):
+            mask = small.tile([P, 16], F32, tag="mask", name="mask_%d" % i)
+            state["mask", i] = mask
+            nc.vector.tensor_scalar(
+                out=mask[:], in0=state["cnt", i][:, 0:16], scalar1=1.0, scalar2=None, op0=ALU.min
+            )
+
+        def mask_mul(i):
+            mask = state["mask", i]
+            view = a_raw[i][:].rearrange("p (j t k) -> p t j k", j=8, t=16, k=64)
+            for t in range(16):
+                nc.vector.tensor_scalar(
+                    out=view[:, t], in0=view[:, t], scalar1=mask[:, t:t + 1], scalar2=None, op0=ALU.mult
+                )
+
+        def transposes(i, j):
+            aw = a_raw[i][:].bitcast(F32)
+            xt = ps_xt.tile([P, 512], F32, tag="xt", name="xt_%d_%d" % (i, j))
+            state["xt", i, j] = xt
+            for kc in range(4):
+                w0 = 512 * j + 256 * (kc // 2) + kc % 2
+                nc.tensor.transpose(xt[:, 128 * kc:128 * (kc + 1)], aw[:, w0:w0 + 255:2], ident[:])
+
+        def exit_a(i, j):
+            if j % 2 == 0:
+                ga = gap.tile([P, 2048], BF16, tag="ga", name="ga_%d_%d" % (i, j // 2), align_bytes=64)
+                state["ga", i, j // 2] = ga
+            ga = state["ga", i, j // 2]
+            dst = ga[:].bitcast(F32)[:, 512 * (j % 2):512 * (j % 2 + 1)]
+            copy = nc.vector.tensor_copy if (i == NB - 1 and j % 2 == 1) else nc.scalar.copy
+            copy(
+                out=dst.rearrange("p (g m u) -> p g m u", g=2, m=128, u=2),
+                in_=state["xt", i, j][:].rearrange("p (g u m) -> p g m u", g=2, u=2, m=128),
+            )
+
+        def quant_a(i, c):
+            if c == 0:
+                state["ac", i] = codes.tile([P, 2048], U32, tag="ac", name="ac_%d" % i, align_bytes=64)
+                state["asc", i] = codes.tile([P, 2048], U8, tag="asc", name="asc_%d" % i, align_bytes=64)
+            nc.vector.quantize_mx(
+                out=state["ac", i][:, 512 * c:512 * (c + 1)].bitcast(FP8X4),
+                scales=state["asc", i][:, 512 * c:512 * (c + 1)],
+                in_=state["ga", i, c][:],
+            )
+
+        def regroup(i, g, h, eng):
+            if ("gb", i, g) not in state:
+                state["gb", i, g] = gbp.tile([P, 4096], BF16, tag="gb", name="gb_%d_%d" % (i, g), align_bytes=64)
+            gb = state["gb", i, g]
+            src = b_raw[i][:, 4096 * g:4096 * (g + 1)].rearrange("q (t n) -> q t n", t=4)
+            if eng == "g":
+                for n0 in range(512 * h, 512 * (h + 1), G_COLS):
+                    nc.gpsimd.tensor_scalar(
+                        out=gb[:, 4 * n0:4 * (n0 + G_COLS)].rearrange("q (n t) -> q n t", t=4),
+                        in0=src[:, :, n0:n0 + G_COLS].rearrange("q t n -> q n t"),
+                        scalar1=1.0, scalar2=0.0, op0=ALU.mult, op1=ALU.add,
+                    )
+            else:
+                dst = gb[:, 2048 * h:2048 * (h + 1)].rearrange("q (c i t) -> q c t i", i=4, t=4)
+                s4 = src[:, :, 512 * h:512 * (h + 1)].rearrange("q t (c i) -> q c t i", i=4)
+                if eng == "s":
+                    nc.scalar.copy(out=dst, in_=s4)
+                else:
+                    nc.vector.tensor_copy(out=dst, in_=s4)
+
+        def quant_b(i, g):
+            if g == 0:
+                state["bc", i] = codes.tile([P, 2048], U32, tag="bc", name="bc_%d" % i, align_bytes=64)
+                state["bsc", i] = codes.tile([P, 2048], U8, tag="bsc", name="bsc_%d" % i, align_bytes=64)
+            nc.vector.quantize_mx(
+                out=state["bc", i][:, 1024 * g:1024 * (g + 1)].bitcast(FP8X4),
+                scales=state["bsc", i][:, 1024 * g:1024 * (g + 1)],
+                in_=state["gb", i, g][:],
+            )
+
+        def multiply(i, j):
+            if j % 2 == 0:
+                state["o", i, j // 2] = outp.tile([P, 2048], F32, tag="o", name="o_%d_%d" % (i, j // 2))
+            o_t = state["o", i, j // 2]
+            for h in range(2):
+                acc = ps_acc.tile([P, 512], F32, tag="acc", name="acc_%d_%d_%d" % (i, j, h))
+                for g in range(2):
+                    lo = 256 * j + 128 * g
+                    ro = 1024 * g + 512 * h
+                    nc.tensor.matmul_mx(
+                        out=acc[:],
+                        lhsT=state["ac", i][:, lo:lo + 128].bitcast(FP8X4),
+                        lhsT_scale=state["asc", i][:, lo:lo + 128],
+                        rhs=state["bc", i][:, ro:ro + 512].bitcast(FP8X4),
+                        rhs_scale=state["bsc", i][:, ro:ro + 512],
+                        start=(g == 0),
+                        stop=(g == 1),
+                    )
+                oo = 1024 * (j % 2) + 512 * h
+                copy = nc.vector.tensor_copy if (i == NB - 1 and h == 1) else nc.scalar.copy
+                copy(out=o_t[:, oo:oo + 512], in_=acc[:])
+            if j % 2 == 1:
+                c = j // 2
+                nc.sync.dma_start(
+                    out=out[i].rearrange("(p j) n -> p (j n)", j=8)[:, 2048 * c:2048 * (c + 1)], in_=o_t[:]
+                )
+
+        def regroup_batch(i, eng):
+            for (g, h), e in zip(((0, 0), (0, 1), (1, 0), (1, 1)), RG[i]):
+                if e == eng:
+                    regroup(i, g, h, e)
+
+        absmax(0, 0)
+        absmax(0, 1)
+        chain_a(0)
+        count(0)
+        regroup_batch(0, "s")
+        regroup_batch(0, "v")
+        chain_b(0)
+        mask_mul(0)
+        for i in range(NB):
+            more = i + 1 < NB
+            for j in range(8):
+                transposes(i, j)
+                exit_a(i, j)
+            if more:
+                absmax(i + 1, 0)
+                regroup_batch(i + 1, "s")
+            quant_b(i, 0)
+            quant_b(i, 1)
+            quant_a(i, 0)
+            quant_a(i, 1)
+            if more:
+                for j in range(4):
+                    multiply(i, j)
+                absmax(i + 1, 1)
+                chain_a(i + 1)
+                count(i + 1)
+                regroup_batch(i + 1, "v")
+            quant_a(i, 2)
+            quant_a(i, 3)
+            if more:
+                chain_b(i + 1)
+                mask_mul(i + 1)
+            for j in range(4 if more else 0, 8):
+                multiply(i, j)
+
+
+RG = (("s", "s", "s", "v"), ("v", "s", "v", "s"), ("v", "s", "v", "s"), ("v", "s", "v", "s"))

@@ -16,225 +16,216 @@ AX = mybir.AxisListType
 
 P = 128
 NB = 4
+NH = 2 * NB
 THRESHOLD = 1e-6
-PIN = False
-G_COLS = 256
 
 
 def tile_sparsebmm_t_kernel(tc, a, b, out):
     nc = tc.nc
     with ExitStack() as ctx:
         const = ctx.enter_context(tc.tile_pool(name="const", bufs=1))
-        raw = ctx.enter_context(tc.tile_pool(name="raw", bufs=3))
-        scr = ctx.enter_context(tc.tile_pool(name="scr", bufs=1))
+        rawa = ctx.enter_context(tc.tile_pool(name="rawa", bufs=5))
+        rawb = ctx.enter_context(tc.tile_pool(name="rawb", bufs=3))
+        scr = ctx.enter_context(tc.tile_pool(name="scr", bufs=2))
         small = ctx.enter_context(tc.tile_pool(name="small", bufs=2))
-        gap = ctx.enter_context(tc.tile_pool(name="gap", bufs=4))
+        gap = ctx.enter_context(tc.tile_pool(name="gap", bufs=3))
         gbp = ctx.enter_context(tc.tile_pool(name="gbp", bufs=4))
         codes = ctx.enter_context(tc.tile_pool(name="codes", bufs=2))
         outp = ctx.enter_context(tc.tile_pool(name="outp", bufs=3))
         ps_xt = ctx.enter_context(tc.psum_pool(name="ps_xt", bufs=3))
         ps_acc = ctx.enter_context(tc.psum_pool(name="ps_acc", bufs=4))
         ps_cnt = ctx.enter_context(tc.psum_pool(name="ps_cnt", bufs=1))
-        if PIN:
-            ctx.enter_context(tc.manual_schedule())
 
         a_raw = []
         b_raw = []
-        for i in range(NB):
-            a_t = raw.tile([P, 8192], BF16, tag="a_raw", name="a_raw%d" % i)
-            b_t = raw.tile([P, 8192], BF16, tag="b_raw", name="b_raw%d" % i)
+
+        def load_a(hf):
+            a_t = rawa.tile([P, 4096], BF16, tag="a_raw", name="a_raw%d" % hf)
             a_raw.append(a_t)
-            b_raw.append(b_t)
-            a_view = a[i].rearrange("(p j) k -> p (j k)", j=8)
-            for c in range(2):
-                nc.sync.dma_start(out=a_t[:, 4096 * c:4096 * (c + 1)], in_=a_view[:, 4096 * c:4096 * (c + 1)])
-            for g in range(2):
-                nc.sync.dma_start(
-                    out=b_t[:, 4096 * g:4096 * (g + 1)],
-                    in_=b[i][512 * g:512 * (g + 1), :].rearrange("(q t) n -> q (t n)", t=4),
-                )
+            view = a[hf // 2][512 * (hf % 2):512 * (hf % 2) + 512, :].rearrange("(p j) k -> p (j k)", j=4)
+            pieces = 2 if hf == 0 else 1
+            w = 4096 // pieces
+            for c in range(pieces):
+                nc.sync.dma_start(out=a_t[:, w * c:w * (c + 1)], in_=view[:, w * c:w * (c + 1)])
+
+        def load_b(i, g):
+            if g == 0:
+                b_t = rawb.tile([P, 8192], BF16, tag="b_raw", name="b_raw%d" % i)
+                b_raw.append(b_t)
+            nc.sync.dma_start(
+                out=b_raw[i][:, 4096 * g:4096 * (g + 1)],
+                in_=b[i][512 * g:512 * (g + 1), :].rearrange("(q t) n -> q (t n)", t=4),
+            )
+
+        for i in range(NB):
+            load_a(2 * i)
+            load_b(i, 0)
+            load_b(i, 1)
+            load_a(2 * i + 1)
 
         ident = const.tile([P, P], F32)
         make_identity(nc, ident[:])
-        blk = const.tile([P, 16], F32)
-        nc.vector.tensor_reduce(out=blk[:], in_=ident[:].rearrange("p (g c) -> p g c", c=8), axis=AX.X, op=ALU.add)
-        group_ones = const.tile([P, P], BF16)
-        nc.vector.tensor_copy(
-            out=group_ones[:].rearrange("p (g c) -> p g c", c=8),
-            in_=blk[:].unsqueeze(2).to_broadcast([P, 16, 8]),
-        )
-        ind = const.tile([P, 32 * NB], BF16)
-        nc.vector.memset(ind[:].bitcast(I32), 0)
+        rows8 = const.tile([P, 8], F32)
+        nc.vector.tensor_reduce(out=rows8[:], in_=ident[:].rearrange("p (g c) -> p g c", c=16), axis=AX.X, op=ALU.add)
+        rowsel = const.tile([P, 8], BF16)
+        nc.vector.tensor_copy(out=rowsel[:], in_=rows8[:])
+        halves = const.tile([P, 2], F32)
+        nc.vector.tensor_reduce(out=halves[:], in_=ident[:].rearrange("p (g c) -> p g c", c=64), axis=AX.X, op=ALU.add)
+        ksel = const.tile([P, 512], BF16)
+        nc.vector.memset(ksel[:].bitcast(I32), 0)
+        for w in range(4):
+            nc.vector.tensor_copy(
+                out=ksel[:, 128 * w + 32 * w:128 * w + 32 * w + 32].rearrange("p (h c) -> p h c", c=16),
+                in_=halves[:].unsqueeze(2).to_broadcast([P, 2, 16]),
+            )
 
         state = {}
 
-        def absmax(i, c):
-            ab = scr.tile([P, 4096], BF16, tag="ab", name="ab_%d_%d" % (i, c))
-            nc.vector.tensor_scalar(
-                out=ab[:].bitcast(I32),
-                in0=a_raw[i][:, 4096 * c:4096 * (c + 1)].bitcast(I32),
-                scalar1=0x7FFF7FFF, scalar2=None, op0=ALU.bitwise_and,
-            )
-            nc.vector.tensor_tensor(out=ab[:, 0:2048], in0=ab[:, 0:2048], in1=ab[:, 2048:4096], op=ALU.max)
-            hm = scr.tile([P, 1024], BF16, tag="hm%d" % c, name="hm_%d_%d" % (i, c))
-            state["hm", i, c] = hm
-            nc.vector.tensor_tensor(out=hm[:], in0=ab[:, 0:1024], in1=ab[:, 1024:2048], op=ALU.max)
-
-        def chain_a(i):
-            h0 = state["hm", i, 0]
-            nc.vector.tensor_tensor(out=h0[:], in0=h0[:], in1=state["hm", i, 1][:], op=ALU.max)
-            rm = small.tile([P, 16], F32, tag="rm", name="rm_%d" % i)
-            nc.vector.tensor_reduce(out=rm[:], in_=h0[:].rearrange("p (t k) -> p t k", k=64), axis=AX.X, op=ALU.max)
-            nc.vector.tensor_scalar(
-                out=ind[:, 32 * i:32 * i + 16], in0=rm[:], scalar1=THRESHOLD, scalar2=None, op0=ALU.is_gt
-            )
-
-        def count(i):
-            cnt = ps_cnt.tile([P, 32], F32, tag="cnt", name="cnt_%d" % i)
-            state["cnt", i] = cnt
-            nc.tensor.matmul(out=cnt[:], lhsT=group_ones[:], rhs=ind[:, 32 * i:32 * (i + 1)], start=True, stop=True)
-
-        def chain_b(i):
-            mask = small.tile([P, 16], F32, tag="mask", name="mask_%d" % i)
-            state["mask", i] = mask
-            nc.vector.tensor_scalar(
-                out=mask[:], in0=state["cnt", i][:, 0:16], scalar1=1.0, scalar2=None, op0=ALU.min
-            )
-
-        def mask_mul(i):
-            mask = state["mask", i]
-            view = a_raw[i][:].rearrange("p (j t k) -> p t j k", j=8, t=16, k=64)
-            for t in range(16):
+        def detect(hf):
+            ab = scr.tile([P, 4096], BF16, tag="ab", name="ab_%d" % hf)
+            pieces = 2 if hf == 0 else 1
+            w = 4096 // pieces
+            for c in range(pieces):
                 nc.vector.tensor_scalar(
-                    out=view[:, t], in0=view[:, t], scalar1=mask[:, t:t + 1], scalar2=None, op0=ALU.mult
+                    out=ab[:, w * c:w * (c + 1)].bitcast(I32),
+                    in0=a_raw[hf][:, w * c:w * (c + 1)].bitcast(I32),
+                    scalar1=0x7FFF7FFF, scalar2=None, op0=ALU.bitwise_and,
+                )
+            mx = scr.tile([P, 2048], BF16, tag="mx", name="mx_%d" % hf)
+            nc.vector.tensor_tensor(out=mx[:], in0=ab[:, 0:2048], in1=ab[:, 2048:4096], op=ALU.max)
+            ind = scr.tile([P, 2048], BF16, tag="ind", name="ind_%d" % hf)
+            nc.vector.tensor_scalar(out=ind[:], in0=mx[:], scalar1=THRESHOLD, scalar2=None, op0=ALU.is_gt)
+            cnt = ps_cnt.tile([P, 80], F32, tag="cnt", name="cnt_%d" % hf)
+            for w in range(8):
+                for jj in range(2):
+                    nc.tensor.matmul(
+                        out=cnt[:, 8 * w:8 * w + 8], lhsT=ind[:, 1024 * jj + 128 * w:1024 * jj + 128 * w + 128],
+                        rhs=rowsel[:], start=(jj == 0), stop=(jj == 1),
+                    )
+            c1 = small.tile([P, 64], BF16, tag="c1", name="c1_%d" % hf)
+            nc.vector.tensor_copy(out=c1[:], in_=cnt[:, 0:64])
+            for w in range(4):
+                nc.tensor.matmul(
+                    out=cnt[:, 64:80], lhsT=ksel[:, 128 * w:128 * (w + 1)],
+                    rhs=c1[:].rearrange("p (g w r) -> p g w r", g=2, w=4)[:, :, w, :],
+                    start=(w == 0), stop=(w == 3),
+                )
+            mask = small.tile([P, 32], BF16, tag="mask", name="mask_%d" % hf)
+            state["mask", hf] = mask
+            nc.vector.tensor_scalar(
+                out=mask[:].rearrange("p (c e) -> p c e", e=2),
+                in0=cnt[:, 64:80].unsqueeze(2).to_broadcast([P, 16, 2]),
+                scalar1=1.0, scalar2=None, op0=ALU.min,
+            )
+
+        def stage_a(hf, j):
+            aw = a_raw[hf][:].bitcast(F32)
+            xt = ps_xt.tile([P, 512], F32, tag="xt", name="xt_%d_%d" % (hf, j))
+            for g in range(2):
+                for u in range(2):
+                    w0 = 512 * j + 256 * g + u
+                    nc.tensor.transpose(
+                        xt[:, 256 * g + 128 * u:256 * g + 128 * (u + 1)], aw[:, w0:w0 + 255:2], ident[:]
+                    )
+            if j % 2 == 0:
+                ga = gap.tile([P, 2048], BF16, tag="ga", name="ga_%d_%d" % (hf, j // 2), align_bytes=64)
+                state["ga", hf, j // 2] = ga
+            ga = state["ga", hf, j // 2]
+            mask = state["mask", hf]
+            for g in range(2):
+                o0 = 1024 * (j % 2) + 512 * g
+                nc.vector.tensor_tensor(
+                    out=ga[:, o0:o0 + 512],
+                    in0=xt[:, 256 * g:256 * (g + 1)].bitcast(BF16).rearrange("q (u m e) -> q m u e", u=2, e=2),
+                    in1=mask[:, 16 * g:16 * (g + 1)].rearrange("q (r e) -> q r e", e=2).unsqueeze(2)
+                    .to_broadcast([P, 8, 32, 2]),
+                    op=ALU.mult,
                 )
 
-        def transposes(i, j):
-            aw = a_raw[i][:].bitcast(F32)
-            xt = ps_xt.tile([P, 512], F32, tag="xt", name="xt_%d_%d" % (i, j))
-            state["xt", i, j] = xt
-            for kc in range(4):
-                w0 = 512 * j + 256 * (kc // 2) + kc % 2
-                nc.tensor.transpose(xt[:, 128 * kc:128 * (kc + 1)], aw[:, w0:w0 + 255:2], ident[:])
-
-        def exit_a(i, j):
-            if j % 2 == 0:
-                ga = gap.tile([P, 2048], BF16, tag="ga", name="ga_%d_%d" % (i, j // 2), align_bytes=64)
-                state["ga", i, j // 2] = ga
-            ga = state["ga", i, j // 2]
-            dst = ga[:].bitcast(F32)[:, 512 * (j % 2):512 * (j % 2 + 1)]
-            copy = nc.vector.tensor_copy if (i == NB - 1 and j % 2 == 1) else nc.scalar.copy
-            copy(
-                out=dst.rearrange("p (g m u) -> p g m u", g=2, m=128, u=2),
-                in_=state["xt", i, j][:].rearrange("p (g u m) -> p g m u", g=2, u=2, m=128),
-            )
-
-        def quant_a(i, c):
+        def quant_a(hf, c):
             if c == 0:
-                state["ac", i] = codes.tile([P, 2048], U32, tag="ac", name="ac_%d" % i, align_bytes=64)
-                state["asc", i] = codes.tile([P, 2048], U8, tag="asc", name="asc_%d" % i, align_bytes=64)
+                state["ac", hf] = codes.tile([P, 1024], U32, tag="ac", name="ac_%d" % hf, align_bytes=64)
+                state["asc", hf] = codes.tile([P, 1024], U8, tag="asc", name="asc_%d" % hf, align_bytes=64)
             nc.vector.quantize_mx(
-                out=state["ac", i][:, 512 * c:512 * (c + 1)].bitcast(FP8X4),
-                scales=state["asc", i][:, 512 * c:512 * (c + 1)],
-                in_=state["ga", i, c][:],
+                out=state["ac", hf][:, 512 * c:512 * (c + 1)].bitcast(FP8X4),
+                scales=state["asc", hf][:, 512 * c:512 * (c + 1)],
+                in_=state["ga", hf, c][:],
             )
 
-        def regroup(i, g, h, eng):
-            if ("gb", i, g) not in state:
-                state["gb", i, g] = gbp.tile([P, 4096], BF16, tag="gb", name="gb_%d_%d" % (i, g), align_bytes=64)
-            gb = state["gb", i, g]
+        def regroup(i, g, h):
+            gb = gbp.tile([P, 2048], BF16, tag="gb", name="gb_%d_%d_%d" % (i, g, h), align_bytes=64)
+            state["gb", i, g, h] = gb
             src = b_raw[i][:, 4096 * g:4096 * (g + 1)].rearrange("q (t n) -> q t n", t=4)
-            if eng == "g":
-                for n0 in range(512 * h, 512 * (h + 1), G_COLS):
-                    nc.gpsimd.tensor_scalar(
-                        out=gb[:, 4 * n0:4 * (n0 + G_COLS)].rearrange("q (n t) -> q n t", t=4),
-                        in0=src[:, :, n0:n0 + G_COLS].rearrange("q t n -> q n t"),
-                        scalar1=1.0, scalar2=0.0, op0=ALU.mult, op1=ALU.add,
-                    )
+            dst = gb[:].rearrange("q (c i t) -> q c t i", i=4, t=4)
+            s4 = src[:, :, 512 * h:512 * (h + 1)].rearrange("q t (c i) -> q c t i", i=4)
+            if (g, h) == (1, 1):
+                nc.vector.tensor_copy(out=dst, in_=s4)
             else:
-                dst = gb[:, 2048 * h:2048 * (h + 1)].rearrange("q (c i t) -> q c t i", i=4, t=4)
-                s4 = src[:, :, 512 * h:512 * (h + 1)].rearrange("q t (c i) -> q c t i", i=4)
-                if eng == "s":
-                    nc.scalar.copy(out=dst, in_=s4)
-                else:
-                    nc.vector.tensor_copy(out=dst, in_=s4)
+                nc.scalar.copy(out=dst, in_=s4)
 
-        def quant_b(i, g):
-            if g == 0:
+        def quant_b(i, g, h):
+            if (g, h) == (0, 0):
                 state["bc", i] = codes.tile([P, 2048], U32, tag="bc", name="bc_%d" % i, align_bytes=64)
                 state["bsc", i] = codes.tile([P, 2048], U8, tag="bsc", name="bsc_%d" % i, align_bytes=64)
+            lo = 1024 * g + 512 * h
             nc.vector.quantize_mx(
-                out=state["bc", i][:, 1024 * g:1024 * (g + 1)].bitcast(FP8X4),
-                scales=state["bsc", i][:, 1024 * g:1024 * (g + 1)],
-                in_=state["gb", i, g][:],
+                out=state["bc", i][:, lo:lo + 512].bitcast(FP8X4),
+                scales=state["bsc", i][:, lo:lo + 512],
+                in_=state["gb", i, g, h][:],
             )
 
-        def multiply(i, j):
+        def multiply(hf, j):
+            i = hf // 2
             if j % 2 == 0:
-                state["o", i, j // 2] = outp.tile([P, 2048], F32, tag="o", name="o_%d_%d" % (i, j // 2))
-            o_t = state["o", i, j // 2]
+                state["o", hf, j // 2] = outp.tile([P, 2048], F32, tag="o", name="o_%d_%d" % (hf, j // 2))
+            o_t = state["o", hf, j // 2]
             for h in range(2):
-                acc = ps_acc.tile([P, 512], F32, tag="acc", name="acc_%d_%d_%d" % (i, j, h))
+                acc = ps_acc.tile([P, 512], F32, tag="acc", name="acc_%d_%d_%d" % (hf, j, h))
                 for g in range(2):
                     lo = 256 * j + 128 * g
                     ro = 1024 * g + 512 * h
                     nc.tensor.matmul_mx(
                         out=acc[:],
-                        lhsT=state["ac", i][:, lo:lo + 128].bitcast(FP8X4),
-                        lhsT_scale=state["asc", i][:, lo:lo + 128],
+                        lhsT=state["ac", hf][:, lo:lo + 128].bitcast(FP8X4),
+                        lhsT_scale=state["asc", hf][:, lo:lo + 128],
                         rhs=state["bc", i][:, ro:ro + 512].bitcast(FP8X4),
                         rhs_scale=state["bsc", i][:, ro:ro + 512],
                         start=(g == 0),
                         stop=(g == 1),
                     )
                 oo = 1024 * (j % 2) + 512 * h
-                copy = nc.vector.tensor_copy if (i == NB - 1 and h == 1) else nc.scalar.copy
-                copy(out=o_t[:, oo:oo + 512], in_=acc[:])
+                nc.scalar.copy(out=o_t[:, oo:oo + 512], in_=acc[:])
             if j % 2 == 1:
                 c = j // 2
                 nc.sync.dma_start(
-                    out=out[i].rearrange("(p j) n -> p (j n)", j=8)[:, 2048 * c:2048 * (c + 1)], in_=o_t[:]
+                    out=out[i][512 * (hf % 2):512 * (hf % 2) + 512, :].rearrange("(p j) n -> p (j n)", j=4)[
+                        :, 2048 * c:2048 * (c + 1)],
+                    in_=o_t[:],
                 )
 
-        def regroup_batch(i, eng):
-            for (g, h), e in zip(((0, 0), (0, 1), (1, 0), (1, 1)), RG[i]):
-                if e == eng:
-                    regroup(i, g, h, e)
-
-        absmax(0, 0)
-        absmax(0, 1)
-        chain_a(0)
-        count(0)
-        regroup_batch(0, "s")
-        regroup_batch(0, "v")
-        chain_b(0)
-        mask_mul(0)
-        for i in range(NB):
-            more = i + 1 < NB
-            for j in range(8):
-                transposes(i, j)
-                exit_a(i, j)
-            if more:
-                absmax(i + 1, 0)
-                regroup_batch(i + 1, "s")
-            quant_b(i, 0)
-            quant_b(i, 1)
-            quant_a(i, 0)
-            quant_a(i, 1)
-            if more:
-                for j in range(4):
-                    multiply(i, j)
-                absmax(i + 1, 1)
-                chain_a(i + 1)
-                count(i + 1)
-                regroup_batch(i + 1, "v")
-            quant_a(i, 2)
-            quant_a(i, 3)
-            if more:
-                chain_b(i + 1)
-                mask_mul(i + 1)
-            for j in range(4 if more else 0, 8):
-                multiply(i, j)
-
-
-RG = (("s", "s", "s", "v"), ("v", "s", "v", "s"), ("v", "s", "v", "s"), ("v", "s", "v", "s"))
+        QUARTERS = ((0, 0), (1, 0), (0, 1), (1, 1))
+        detect(0)
+        for g, h in QUARTERS:
+            regroup(0, g, h)
+        for j in range(4):
+            stage_a(0, j)
+            if j % 2 == 1:
+                quant_a(0, j // 2)
+        for g, h in QUARTERS:
+            quant_b(0, g, h)
+        detect(1)
+        for hf in range(NH):
+            for c in range(2):
+                multiply(hf, 2 * c)
+                multiply(hf, 2 * c + 1)
+                if hf // 2 + 1 < NB:
+                    g, h = QUARTERS[2 * (hf % 2) + c]
+                    regroup(hf // 2 + 1, g, h)
+                if hf + 1 < NH:
+                    stage_a(hf + 1, 2 * c)
+                    stage_a(hf + 1, 2 * c + 1)
+                    quant_a(hf + 1, c)
+                if c == 0 and hf + 2 < NH:
+                    detect(hf + 2)
+                if hf // 2 + 1 < NB:
+                    quant_b(hf // 2 + 1, g, h)

@@ -24,14 +24,14 @@ def tile_sparsebmm_t_kernel(tc, a, b, out):
     nc = tc.nc
     with ExitStack() as ctx:
         const = ctx.enter_context(tc.tile_pool(name="const", bufs=1))
-        rawa = ctx.enter_context(tc.tile_pool(name="rawa", bufs=5))
-        rawb = ctx.enter_context(tc.tile_pool(name="rawb", bufs=3))
+        rawa = ctx.enter_context(tc.tile_pool(name="rawa", bufs=4))
+        rawb = ctx.enter_context(tc.tile_pool(name="rawb", bufs=2))
         scr = ctx.enter_context(tc.tile_pool(name="scr", bufs=2))
         small = ctx.enter_context(tc.tile_pool(name="small", bufs=2))
         gap = ctx.enter_context(tc.tile_pool(name="gap", bufs=3))
         gbp = ctx.enter_context(tc.tile_pool(name="gbp", bufs=4))
         codes = ctx.enter_context(tc.tile_pool(name="codes", bufs=2))
-        outp = ctx.enter_context(tc.tile_pool(name="outp", bufs=3))
+        outp = ctx.enter_context(tc.tile_pool(name="outp", bufs=5))
         ps_xt = ctx.enter_context(tc.psum_pool(name="ps_xt", bufs=3))
         ps_acc = ctx.enter_context(tc.psum_pool(name="ps_acc", bufs=4))
         ps_cnt = ctx.enter_context(tc.psum_pool(name="ps_cnt", bufs=1))

@@ -18,6 +18,7 @@ P = 128
 NB = 4
 NH = 2 * NB
 THRESHOLD = 1e-6
+HEAD_PIECES = 2
 
 
 def tile_sparsebmm_t_kernel(tc, a, b, out):
@@ -31,44 +32,65 @@ def tile_sparsebmm_t_kernel(tc, a, b, out):
         gap = ctx.enter_context(tc.tile_pool(name="gap", bufs=3))
         gbp = ctx.enter_context(tc.tile_pool(name="gbp", bufs=4))
         codes = ctx.enter_context(tc.tile_pool(name="codes", bufs=2))
-        outp = ctx.enter_context(tc.tile_pool(name="outp", bufs=5))
+        outp = ctx.enter_context(tc.tile_pool(name="outp", bufs=4))
         ps_xt = ctx.enter_context(tc.psum_pool(name="ps_xt", bufs=3))
         ps_acc = ctx.enter_context(tc.psum_pool(name="ps_acc", bufs=4))
         ps_cnt = ctx.enter_context(tc.psum_pool(name="ps_cnt", bufs=1))
 
-        a_raw = []
-        b_raw = []
+
+        ctx.enter_context(tc.manual_schedule())
+        a_raw = {}
+        b_raw = {}
 
         def load_a(hf):
+            if hf >= NH:
+                return
             a_t = rawa.tile([P, 4096], BF16, tag="a_raw", name="a_raw%d" % hf)
-            a_raw.append(a_t)
+            a_raw[hf] = a_t
             view = a[hf // 2][512 * (hf % 2):512 * (hf % 2) + 512, :].rearrange("(p j) k -> p (j k)", j=4)
-            pieces = 2 if hf == 0 else 1
+            pieces = HEAD_PIECES if hf == 0 else 1
             w = 4096 // pieces
             for c in range(pieces):
                 nc.sync.dma_start(out=a_t[:, w * c:w * (c + 1)], in_=view[:, w * c:w * (c + 1)])
 
-        def load_b(i, g):
-            if g == 0:
-                b_t = rawb.tile([P, 8192], BF16, tag="b_raw", name="b_raw%d" % i)
-                b_raw.append(b_t)
+        def new_b(i):
+            b_t = rawb.tile([P, 8192], BF16, tag="b_raw", name="b_raw%d" % i)
+            b_raw[i] = b_t
+
+        def load_b(i):
+            if i >= NB:
+                return
+            new_b(i)
+            for g in range(2):
+                nc.sync.dma_start(
+                    out=b_raw[i][:, 4096 * g:4096 * (g + 1)],
+                    in_=b[i][512 * g:512 * (g + 1), :].rearrange("(q t) n -> q (t n)", t=4),
+                )
+
+        def load_b_quarter(g, h):
+            lo = 4096 * g + 2048 * h
             nc.sync.dma_start(
-                out=b_raw[i][:, 4096 * g:4096 * (g + 1)],
-                in_=b[i][512 * g:512 * (g + 1), :].rearrange("(q t) n -> q (t n)", t=4),
+                out=b_raw[0][:, lo:lo + 2048].rearrange("q (t n) -> q t n", t=4),
+                in_=b[0][512 * g:512 * (g + 1), 512 * h:512 * (h + 1)].rearrange("(q t) n -> q t n", t=4),
             )
 
-        for i in range(NB):
-            load_a(2 * i)
-            load_b(i, 0)
-            load_b(i, 1)
-            load_a(2 * i + 1)
+        new_b(0)
+        load_a(0)
+        load_b_quarter(0, 0)
+        load_a(1)
+        load_b_quarter(1, 0)
+        load_b_quarter(0, 1)
+        load_b_quarter(1, 1)
+        load_a(2)
+        load_b(1)
+        load_a(3)
 
         ident = const.tile([P, P], F32)
         make_identity(nc, ident[:])
         rows8 = const.tile([P, 8], F32)
         nc.vector.tensor_reduce(out=rows8[:], in_=ident[:].rearrange("p (g c) -> p g c", c=16), axis=AX.X, op=ALU.add)
         rowsel = const.tile([P, 8], BF16)
-        nc.vector.tensor_copy(out=rowsel[:], in_=rows8[:])
+        nc.scalar.copy(out=rowsel[:], in_=rows8[:])
         halves = const.tile([P, 2], F32)
         nc.vector.tensor_reduce(out=halves[:], in_=ident[:].rearrange("p (g c) -> p g c", c=64), axis=AX.X, op=ALU.add)
         ksel = const.tile([P, 512], BF16)
@@ -79,11 +101,15 @@ def tile_sparsebmm_t_kernel(tc, a, b, out):
                 in_=halves[:].unsqueeze(2).to_broadcast([P, 2, 16]),
             )
 
+
         state = {}
 
-        def detect(hf):
+        def absolute(hf):
+            if hf >= NH:
+                return
             ab = scr.tile([P, 4096], BF16, tag="ab", name="ab_%d" % hf)
-            pieces = 2 if hf == 0 else 1
+            state["ab", hf] = ab
+            pieces = HEAD_PIECES if hf == 0 else 1
             w = 4096 // pieces
             for c in range(pieces):
                 nc.vector.tensor_scalar(
@@ -91,58 +117,94 @@ def tile_sparsebmm_t_kernel(tc, a, b, out):
                     in0=a_raw[hf][:, w * c:w * (c + 1)].bitcast(I32),
                     scalar1=0x7FFF7FFF, scalar2=None, op0=ALU.bitwise_and,
                 )
+
+        def fold(hf):
+            if hf >= NH:
+                return
+            ab = state["ab", hf]
             mx = scr.tile([P, 2048], BF16, tag="mx", name="mx_%d" % hf)
+            state["mx", hf] = mx
             nc.vector.tensor_tensor(out=mx[:], in0=ab[:, 0:2048], in1=ab[:, 2048:4096], op=ALU.max)
+
+        def indicate(hf):
+            if hf >= NH:
+                return
             ind = scr.tile([P, 2048], BF16, tag="ind", name="ind_%d" % hf)
-            nc.vector.tensor_scalar(out=ind[:], in0=mx[:], scalar1=THRESHOLD, scalar2=None, op0=ALU.is_gt)
+            state["ind", hf] = ind
+            nc.vector.tensor_scalar(
+                out=ind[:], in0=state["mx", hf][:], scalar1=THRESHOLD, scalar2=None, op0=ALU.is_gt)
+
+        def count_rows(hf):
+            if hf >= NH:
+                return
             cnt = ps_cnt.tile([P, 80], F32, tag="cnt", name="cnt_%d" % hf)
+            state["cnt", hf] = cnt
+            ind = state["ind", hf]
             for w in range(8):
                 for jj in range(2):
                     nc.tensor.matmul(
                         out=cnt[:, 8 * w:8 * w + 8], lhsT=ind[:, 1024 * jj + 128 * w:1024 * jj + 128 * w + 128],
                         rhs=rowsel[:], start=(jj == 0), stop=(jj == 1),
                     )
+
+        def counts_out(hf):
+            if hf >= NH:
+                return
             c1 = small.tile([P, 64], BF16, tag="c1", name="c1_%d" % hf)
-            nc.vector.tensor_copy(out=c1[:], in_=cnt[:, 0:64])
+            state["c1", hf] = c1
+            nc.vector.tensor_copy(out=c1[:], in_=state["cnt", hf][:, 0:64])
+
+        def count_tiles(hf):
+            if hf >= NH:
+                return
+            c1 = state["c1", hf]
             for w in range(4):
                 nc.tensor.matmul(
-                    out=cnt[:, 64:80], lhsT=ksel[:, 128 * w:128 * (w + 1)],
+                    out=state["cnt", hf][:, 64:80], lhsT=ksel[:, 128 * w:128 * (w + 1)],
                     rhs=c1[:].rearrange("p (g w r) -> p g w r", g=2, w=4)[:, :, w, :],
                     start=(w == 0), stop=(w == 3),
                 )
+
+        def make_mask(hf):
+            if hf >= NH:
+                return
             mask = small.tile([P, 32], BF16, tag="mask", name="mask_%d" % hf)
             state["mask", hf] = mask
             nc.vector.tensor_scalar(
                 out=mask[:].rearrange("p (c e) -> p c e", e=2),
-                in0=cnt[:, 64:80].unsqueeze(2).to_broadcast([P, 16, 2]),
+                in0=state["cnt", hf][:, 64:80].unsqueeze(2).to_broadcast([P, 16, 2]),
                 scalar1=1.0, scalar2=None, op0=ALU.min,
             )
 
-        def stage_a(hf, j):
+        def transpose_a(hf, j):
+            if hf >= NH:
+                return
             aw = a_raw[hf][:].bitcast(F32)
             xt = ps_xt.tile([P, 512], F32, tag="xt", name="xt_%d_%d" % (hf, j))
+            state["xt", hf, j] = xt
             for g in range(2):
                 for u in range(2):
                     w0 = 512 * j + 256 * g + u
                     nc.tensor.transpose(
-                        xt[:, 256 * g + 128 * u:256 * g + 128 * (u + 1)], aw[:, w0:w0 + 255:2], ident[:]
+                        xt[:, 256 * u + 128 * g:256 * u + 128 * (g + 1)], aw[:, w0:w0 + 255:2], ident[:]
                     )
+
+        def masked_copy(hf, j):
+            if hf >= NH:
+                return
             if j % 2 == 0:
                 ga = gap.tile([P, 2048], BF16, tag="ga", name="ga_%d_%d" % (hf, j // 2), align_bytes=64)
                 state["ga", hf, j // 2] = ga
-            ga = state["ga", hf, j // 2]
-            mask = state["mask", hf]
-            for g in range(2):
-                o0 = 1024 * (j % 2) + 512 * g
-                nc.vector.tensor_tensor(
-                    out=ga[:, o0:o0 + 512],
-                    in0=xt[:, 256 * g:256 * (g + 1)].bitcast(BF16).rearrange("q (u m e) -> q m u e", u=2, e=2),
-                    in1=mask[:, 16 * g:16 * (g + 1)].rearrange("q (r e) -> q r e", e=2).unsqueeze(2)
-                    .to_broadcast([P, 8, 32, 2]),
-                    op=ALU.mult,
-                )
+            nc.vector.tensor_tensor(
+                out=state["ga", hf, j // 2][:, 1024 * (j % 2):1024 * (j % 2 + 1)],
+                in0=state["xt", hf, j][:].bitcast(BF16).rearrange("q (u m e) -> q m u e", u=2, e=2),
+                in1=state["mask", hf][:].rearrange("q (r e) -> q r e", e=2).unsqueeze(2).to_broadcast([P, 16, 32, 2]),
+                op=ALU.mult,
+            )
 
         def quant_a(hf, c):
+            if hf >= NH:
+                return
             if c == 0:
                 state["ac", hf] = codes.tile([P, 1024], U32, tag="ac", name="ac_%d" % hf, align_bytes=64)
                 state["asc", hf] = codes.tile([P, 1024], U8, tag="asc", name="asc_%d" % hf, align_bytes=64)
@@ -152,18 +214,27 @@ def tile_sparsebmm_t_kernel(tc, a, b, out):
                 in_=state["ga", hf, c][:],
             )
 
-        def regroup(i, g, h):
-            gb = gbp.tile([P, 2048], BF16, tag="gb", name="gb_%d_%d_%d" % (i, g, h), align_bytes=64)
-            state["gb", i, g, h] = gb
-            src = b_raw[i][:, 4096 * g:4096 * (g + 1)].rearrange("q (t n) -> q t n", t=4)
-            dst = gb[:].rearrange("q (c i t) -> q c t i", i=4, t=4)
-            s4 = src[:, :, 512 * h:512 * (h + 1)].rearrange("q t (c i) -> q c t i", i=4)
-            if (g, h) == (1, 1):
-                nc.vector.tensor_copy(out=dst, in_=s4)
+        def regroup(i, g, h, copy, lo4=0, hi4=128):
+            if i >= NB:
+                return
+            if ("gb", i, g, h) not in state:
+                state["gb", i, g, h] = gbp.tile(
+                    [P, 2048], BF16, tag="gb", name="gb_%d_%d_%d" % (i, g, h), align_bytes=64)
+            gb = state["gb", i, g, h]
+            if i == 0:
+                lo = 4096 * g + 2048 * h
+                src = b_raw[0][:, lo:lo + 2048].rearrange("q (t n) -> q t n", t=4)
             else:
-                nc.scalar.copy(out=dst, in_=s4)
+                src = b_raw[i][:, 4096 * g:4096 * (g + 1)].rearrange(
+                    "q (t n) -> q t n", t=4)[:, :, 512 * h:512 * (h + 1)]
+            copy(
+                out=gb[:].rearrange("q (c i t) -> q c t i", i=4, t=4)[:, lo4:hi4],
+                in_=src.rearrange("q t (c i) -> q c t i", i=4)[:, lo4:hi4],
+            )
 
         def quant_b(i, g, h):
+            if i >= NB:
+                return
             if (g, h) == (0, 0):
                 state["bc", i] = codes.tile([P, 2048], U32, tag="bc", name="bc_%d" % i, align_bytes=64)
                 state["bsc", i] = codes.tile([P, 2048], U8, tag="bsc", name="bsc_%d" % i, align_bytes=64)
@@ -174,58 +245,122 @@ def tile_sparsebmm_t_kernel(tc, a, b, out):
                 in_=state["gb", i, g, h][:],
             )
 
-        def multiply(hf, j):
+        def multiply(hf, c, j, h):
             i = hf // 2
-            if j % 2 == 0:
-                state["o", hf, j // 2] = outp.tile([P, 2048], F32, tag="o", name="o_%d_%d" % (hf, j // 2))
-            o_t = state["o", hf, j // 2]
-            for h in range(2):
-                acc = ps_acc.tile([P, 512], F32, tag="acc", name="acc_%d_%d_%d" % (hf, j, h))
-                for g in range(2):
-                    lo = 256 * j + 128 * g
-                    ro = 1024 * g + 512 * h
-                    nc.tensor.matmul_mx(
-                        out=acc[:],
-                        lhsT=state["ac", hf][:, lo:lo + 128].bitcast(FP8X4),
-                        lhsT_scale=state["asc", hf][:, lo:lo + 128],
-                        rhs=state["bc", i][:, ro:ro + 512].bitcast(FP8X4),
-                        rhs_scale=state["bsc", i][:, ro:ro + 512],
-                        start=(g == 0),
-                        stop=(g == 1),
-                    )
-                oo = 1024 * (j % 2) + 512 * h
-                nc.scalar.copy(out=o_t[:, oo:oo + 512], in_=acc[:])
-            if j % 2 == 1:
-                c = j // 2
-                nc.sync.dma_start(
-                    out=out[i][512 * (hf % 2):512 * (hf % 2) + 512, :].rearrange("(p j) n -> p (j n)", j=4)[
-                        :, 2048 * c:2048 * (c + 1)],
-                    in_=o_t[:],
+            acc = ps_acc.tile([P, 512], F32, tag="acc", name="acc_%d_%d_%d_%d" % (hf, c, j, h))
+            state["acc", hf, c, j, h] = acc
+            for g in range(2):
+                lo = 512 * c + 256 * j + 128 * g
+                ro = 1024 * g + 512 * h
+                nc.tensor.matmul_mx(
+                    out=acc[:],
+                    lhsT=state["ac", hf][:, lo:lo + 128].bitcast(FP8X4),
+                    lhsT_scale=state["asc", hf][:, lo:lo + 128],
+                    rhs=state["bc", i][:, ro:ro + 512].bitcast(FP8X4),
+                    rhs_scale=state["bsc", i][:, ro:ro + 512],
+                    start=(g == 0),
+                    stop=(g == 1),
                 )
 
-        QUARTERS = ((0, 0), (1, 0), (0, 1), (1, 1))
-        detect(0)
-        for g, h in QUARTERS:
-            regroup(0, g, h)
-        for j in range(4):
-            stage_a(0, j)
-            if j % 2 == 1:
-                quant_a(0, j // 2)
-        for g, h in QUARTERS:
-            quant_b(0, g, h)
-        detect(1)
+        def copy_out(hf, c, j, h, copy):
+            if ("o", hf, c) not in state:
+                state["o", hf, c] = outp.tile([P, 2048], F32, tag="o", name="o_%d_%d" % (hf, c))
+            oo = 1024 * j + 512 * h
+            copy(out=state["o", hf, c][:, oo:oo + 512], in_=state["acc", hf, c, j, h][:])
+
+        def store(hf, c, lo, hi):
+            dst = out[hf // 2][512 * (hf % 2):512 * (hf % 2) + 512, :].rearrange("(p j) n -> p (j n)", j=4)
+            nc.sync.dma_start(out=dst[:, 2048 * c + lo:2048 * c + hi], in_=state["o", hf, c][:, lo:hi])
+
+        scopy = nc.scalar.copy
+        vcopy = nc.vector.tensor_copy
+
+        def products(hf, group):
+            for c, j, h in group:
+                multiply(hf, c, j, h)
+                copy_out(hf, c, j, h, vcopy if hf == NH - 1 and h == 1 else scopy)
+
+        for g, h in ((0, 0), (1, 0), (0, 1), (1, 1)):
+            regroup(0, g, h, scopy)
+        for j in range(3):
+            transpose_a(0, j)
+        absolute(0)
+        fold(0)
+        indicate(0)
+        count_rows(0)
+        absolute(1)
+        counts_out(0)
+        count_tiles(0)
+        fold(1)
+        make_mask(0)
+        masked_copy(0, 0)
+        masked_copy(0, 1)
+        transpose_a(0, 3)
+        indicate(1)
+        quant_a(0, 0)
+        quant_b(0, 0, 0)
+        quant_b(0, 1, 0)
+        count_rows(1)
+        masked_copy(0, 2)
+        masked_copy(0, 3)
+        counts_out(1)
+        count_tiles(1)
+        quant_a(0, 1)
+        make_mask(1)
+        quant_b(0, 0, 1)
+
+        late = (0, 1, 1)
         for hf in range(NH):
-            for c in range(2):
-                multiply(hf, 2 * c)
-                multiply(hf, 2 * c + 1)
-                if hf // 2 + 1 < NB:
-                    g, h = QUARTERS[2 * (hf % 2) + c]
-                    regroup(hf // 2 + 1, g, h)
-                if hf + 1 < NH:
-                    stage_a(hf + 1, 2 * c)
-                    stage_a(hf + 1, 2 * c + 1)
-                    quant_a(hf + 1, c)
-                if c == 0 and hf + 2 < NH:
-                    detect(hf + 2)
-                if hf // 2 + 1 < NB:
-                    quant_b(hf // 2 + 1, g, h)
+            nb = hf // 2 + 1
+            hb = hf % 2
+            last = hf == NH - 1
+            quant_b(*late)
+            if hf == 0:
+                products(0, ((0, 0, 0), (0, 1, 0)))
+                transpose_a(1, 0)
+                transpose_a(1, 1)
+                products(0, ((1, 0, 0), (1, 1, 0)))
+            elif last:
+                products(hf, ((0, 0, 0), (0, 0, 1), (0, 1, 0), (0, 1, 1)))
+                store(hf, 0, 0, 2048)
+            else:
+                products(hf, ((0, 0, 0), (0, 1, 0), (0, 0, 1), (0, 1, 1)))
+                store(hf, 0, 0, 2048)
+            load_a(hf + 4)
+            if hb == 0:
+                load_b(nb + 1)
+            transpose_a(hf + 1, 2)
+            transpose_a(hf + 1, 3)
+            masked_copy(hf + 1, 0)
+            absolute(hf + 2)
+            masked_copy(hf + 1, 1)
+            fold(hf + 2)
+            quant_a(hf + 1, 0)
+            indicate(hf + 2)
+            regroup(nb, 0, hb, scopy)
+            if hf == 0:
+                products(0, ((0, 0, 1), (0, 1, 1)))
+                store(hf, 0, 0, 2048)
+                products(0, ((1, 0, 1), (1, 1, 1)))
+                store(hf, 1, 0, 2048)
+            elif last:
+                products(hf, ((1, 0, 0), (1, 0, 1)))
+                store(hf, 1, 0, 1024)
+                products(hf, ((1, 1, 0), (1, 1, 1)))
+                store(hf, 1, 1024, 2048)
+            else:
+                products(hf, ((1, 0, 0), (1, 1, 0), (1, 0, 1), (1, 1, 1)))
+                store(hf, 1, 0, 2048)
+            masked_copy(hf + 1, 2)
+            masked_copy(hf + 1, 3)
+            regroup(nb, 1, hb, vcopy, 64, 128)
+            regroup(nb, 1, hb, scopy, 0, 64)
+            count_rows(hf + 2)
+            transpose_a(hf + 2, 0)
+            counts_out(hf + 2)
+            quant_a(hf + 1, 1)
+            count_tiles(hf + 2)
+            transpose_a(hf + 2, 1)
+            quant_b(nb, 0, hb)
+            make_mask(hf + 2)
+            late = (nb, 1, hb)

@@ -25,14 +25,14 @@ def tile_sparsebmm_t_kernel(tc, a, b, out):
     nc = tc.nc
     with ExitStack() as ctx:
         const = ctx.enter_context(tc.tile_pool(name="const", bufs=1))
-        rawa = ctx.enter_context(tc.tile_pool(name="rawa", bufs=4))
+        rawa = ctx.enter_context(tc.tile_pool(name="rawa", bufs=5))
         rawb = ctx.enter_context(tc.tile_pool(name="rawb", bufs=2))
         scr = ctx.enter_context(tc.tile_pool(name="scr", bufs=2))
         small = ctx.enter_context(tc.tile_pool(name="small", bufs=2))
         gap = ctx.enter_context(tc.tile_pool(name="gap", bufs=3))
         gbp = ctx.enter_context(tc.tile_pool(name="gbp", bufs=4))
         codes = ctx.enter_context(tc.tile_pool(name="codes", bufs=2))
-        outp = ctx.enter_context(tc.tile_pool(name="outp", bufs=4))
+        outp = ctx.enter_context(tc.tile_pool(name="outp", bufs=5))
         ps_xt = ctx.enter_context(tc.psum_pool(name="ps_xt", bufs=3))
         ps_acc = ctx.enter_context(tc.psum_pool(name="ps_acc", bufs=4))
         ps_cnt = ctx.enter_context(tc.psum_pool(name="ps_cnt", bufs=1))
@@ -126,13 +126,21 @@ def tile_sparsebmm_t_kernel(tc, a, b, out):
             state["mx", hf] = mx
             nc.vector.tensor_tensor(out=mx[:], in0=ab[:, 0:2048], in1=ab[:, 2048:4096], op=ALU.max)
 
+        def fold_again(hf):
+            if hf >= NH:
+                return
+            mx = state["mx", hf]
+            mx2 = scr.tile([P, 1024], BF16, tag="mx2", name="mx2_%d" % hf)
+            state["mx2", hf] = mx2
+            nc.vector.tensor_tensor(out=mx2[:], in0=mx[:, 0:1024], in1=mx[:, 1024:2048], op=ALU.max)
+
         def indicate(hf):
             if hf >= NH:
                 return
-            ind = scr.tile([P, 2048], BF16, tag="ind", name="ind_%d" % hf)
+            ind = scr.tile([P, 1024], BF16, tag="ind", name="ind_%d" % hf)
             state["ind", hf] = ind
             nc.vector.tensor_scalar(
-                out=ind[:], in0=state["mx", hf][:], scalar1=THRESHOLD, scalar2=None, op0=ALU.is_gt)
+                out=ind[:], in0=state["mx2", hf][:], scalar1=THRESHOLD, scalar2=None, op0=ALU.is_gt)
 
         def count_rows(hf):
             if hf >= NH:
@@ -141,11 +149,10 @@ def tile_sparsebmm_t_kernel(tc, a, b, out):
             state["cnt", hf] = cnt
             ind = state["ind", hf]
             for w in range(8):
-                for jj in range(2):
-                    nc.tensor.matmul(
-                        out=cnt[:, 8 * w:8 * w + 8], lhsT=ind[:, 1024 * jj + 128 * w:1024 * jj + 128 * w + 128],
-                        rhs=rowsel[:], start=(jj == 0), stop=(jj == 1),
-                    )
+                nc.tensor.matmul(
+                    out=cnt[:, 8 * w:8 * w + 8], lhsT=ind[:, 128 * w:128 * w + 128], rhs=rowsel[:],
+                    start=True, stop=True,
+                )
 
         def counts_out(hf):
             if hf >= NH:
@@ -286,6 +293,7 @@ def tile_sparsebmm_t_kernel(tc, a, b, out):
             transpose_a(0, j)
         absolute(0)
         fold(0)
+        fold_again(0)
         indicate(0)
         count_rows(0)
         absolute(1)
@@ -294,6 +302,7 @@ def tile_sparsebmm_t_kernel(tc, a, b, out):
         fold(1)
         make_mask(0)
         masked_copy(0, 0)
+        fold_again(1)
         masked_copy(0, 1)
         transpose_a(0, 3)
         indicate(1)
@@ -308,6 +317,7 @@ def tile_sparsebmm_t_kernel(tc, a, b, out):
         quant_a(0, 1)
         make_mask(1)
         quant_b(0, 0, 1)
+        absolute(2)
 
         late = (0, 1, 1)
         for hf in range(NH):
@@ -315,49 +325,53 @@ def tile_sparsebmm_t_kernel(tc, a, b, out):
             hb = hf % 2
             last = hf == NH - 1
             quant_b(*late)
+            load_a(hf + 4)
+            if hb == 0:
+                load_b(nb + 1)
             if hf == 0:
                 products(0, ((0, 0, 0), (0, 1, 0)))
                 transpose_a(1, 0)
                 transpose_a(1, 1)
-                products(0, ((1, 0, 0), (1, 1, 0)))
+                products(0, ((1, 0, 0),))
             elif last:
-                products(hf, ((0, 0, 0), (0, 0, 1), (0, 1, 0), (0, 1, 1)))
-                store(hf, 0, 0, 2048)
+                products(hf, ((0, 0, 0), (0, 0, 1), (0, 1, 0)))
             else:
-                products(hf, ((0, 0, 0), (0, 1, 0), (0, 0, 1), (0, 1, 1)))
-                store(hf, 0, 0, 2048)
-            load_a(hf + 4)
-            if hb == 0:
-                load_b(nb + 1)
+                products(hf, ((0, 0, 0), (0, 1, 0), (0, 0, 1)))
+            masked_copy(hf + 1, 0)
+            fold(hf + 2)
+            masked_copy(hf + 1, 1)
             transpose_a(hf + 1, 2)
             transpose_a(hf + 1, 3)
-            masked_copy(hf + 1, 0)
-            absolute(hf + 2)
-            masked_copy(hf + 1, 1)
-            fold(hf + 2)
+            fold_again(hf + 2)
             quant_a(hf + 1, 0)
             indicate(hf + 2)
             regroup(nb, 0, hb, scopy)
             if hf == 0:
-                products(0, ((0, 0, 1), (0, 1, 1)))
-                store(hf, 0, 0, 2048)
-                products(0, ((1, 0, 1), (1, 1, 1)))
-                store(hf, 1, 0, 2048)
+                products(0, ((1, 1, 0), (0, 0, 1), (0, 1, 1)))
+                store(0, 0, 0, 2048)
             elif last:
+                products(hf, ((0, 1, 1),))
+                store(hf, 0, 0, 2048)
                 products(hf, ((1, 0, 0), (1, 0, 1)))
                 store(hf, 1, 0, 1024)
+            else:
+                products(hf, ((0, 1, 1),))
+                store(hf, 0, 0, 2048)
+                products(hf, ((1, 0, 0), (1, 1, 0)))
+            masked_copy(hf + 1, 2)
+            masked_copy(hf + 1, 3)
+            absolute(hf + 3)
+            count_rows(hf + 2)
+            transpose_a(hf + 2, 0)
+            regroup(nb, 1, hb, vcopy, 64, 128)
+            regroup(nb, 1, hb, scopy, 0, 64)
+            counts_out(hf + 2)
+            if last:
                 products(hf, ((1, 1, 0), (1, 1, 1)))
                 store(hf, 1, 1024, 2048)
             else:
-                products(hf, ((1, 0, 0), (1, 1, 0), (1, 0, 1), (1, 1, 1)))
+                products(hf, ((1, 0, 1), (1, 1, 1)))
                 store(hf, 1, 0, 2048)
-            masked_copy(hf + 1, 2)
-            masked_copy(hf + 1, 3)
-            regroup(nb, 1, hb, vcopy, 64, 128)
-            regroup(nb, 1, hb, scopy, 0, 64)
-            count_rows(hf + 2)
-            transpose_a(hf + 2, 0)
-            counts_out(hf + 2)
             quant_a(hf + 1, 1)
             count_tiles(hf + 2)
             transpose_a(hf + 2, 1)

@@ -19,22 +19,23 @@ NB = 4
 NH = 2 * NB
 THRESHOLD = 1e-6
 HEAD_PIECES = 2
+SPLIT = 56
 
 
 def tile_sparsebmm_t_kernel(tc, a, b, out):
     nc = tc.nc
     with ExitStack() as ctx:
         const = ctx.enter_context(tc.tile_pool(name="const", bufs=1))
-        rawa = ctx.enter_context(tc.tile_pool(name="rawa", bufs=5))
+        rawa = ctx.enter_context(tc.tile_pool(name="rawa", bufs=6))
         rawb = ctx.enter_context(tc.tile_pool(name="rawb", bufs=2))
         scr = ctx.enter_context(tc.tile_pool(name="scr", bufs=2))
         small = ctx.enter_context(tc.tile_pool(name="small", bufs=2))
         gap = ctx.enter_context(tc.tile_pool(name="gap", bufs=3))
         gbp = ctx.enter_context(tc.tile_pool(name="gbp", bufs=4))
         codes = ctx.enter_context(tc.tile_pool(name="codes", bufs=2))
-        outp = ctx.enter_context(tc.tile_pool(name="outp", bufs=5))
-        ps_xt = ctx.enter_context(tc.psum_pool(name="ps_xt", bufs=3))
-        ps_acc = ctx.enter_context(tc.psum_pool(name="ps_acc", bufs=4))
+        outp = ctx.enter_context(tc.tile_pool(name="outp", bufs=4))
+        ps_xt = ctx.enter_context(tc.psum_pool(name="ps_xt", bufs=4))
+        ps_acc = ctx.enter_context(tc.psum_pool(name="ps_acc", bufs=3))
         ps_cnt = ctx.enter_context(tc.psum_pool(name="ps_cnt", bufs=1))
 
 
@@ -84,6 +85,7 @@ def tile_sparsebmm_t_kernel(tc, a, b, out):
         load_a(2)
         load_b(1)
         load_a(3)
+        load_a(4)
 
         ident = const.tile([P, P], F32)
         make_identity(nc, ident[:])
@@ -183,6 +185,15 @@ def tile_sparsebmm_t_kernel(tc, a, b, out):
                 scalar1=1.0, scalar2=None, op0=ALU.min,
             )
 
+        def gate(hf):
+            if hf >= NH:
+                return
+            one = small.tile([P, 1], F32, tag="one", name="one_%d" % hf)
+            state["one", hf] = one
+            nc.vector.tensor_scalar(
+                out=one[:], in0=state["mask", hf][:, 0:1], scalar1=0.0, scalar2=1.0, op0=ALU.mult, op1=ALU.add
+            )
+
         def transpose_a(hf, j):
             if hf >= NH:
                 return
@@ -239,6 +250,21 @@ def tile_sparsebmm_t_kernel(tc, a, b, out):
                 in_=src.rearrange("q t (c i) -> q c t i", i=4)[:, lo4:hi4],
             )
 
+        def regroup_g(i, g, h, lo4, hi4, hf):
+            if i >= NB:
+                return
+            if ("gb", i, g, h) not in state:
+                state["gb", i, g, h] = gbp.tile(
+                    [P, 2048], BF16, tag="gb", name="gb_%d_%d_%d" % (i, g, h), align_bytes=64)
+            gb = state["gb", i, g, h]
+            src = b_raw[i][:, 4096 * g:4096 * (g + 1)].rearrange(
+                "q (t n) -> q t n", t=4)[:, :, 512 * h:512 * (h + 1)]
+            nc.gpsimd.tensor_scalar(
+                out=gb[:].rearrange("q (n t) -> q n t", t=4)[:, 4 * lo4:4 * hi4],
+                in0=src.rearrange("q t n -> q n t")[:, 4 * lo4:4 * hi4],
+                scalar1=state["one", hf][:], scalar2=0.0, op0=ALU.mult, op1=ALU.add,
+            )
+
         def quant_b(i, g, h):
             if i >= NB:
                 return
@@ -289,7 +315,7 @@ def tile_sparsebmm_t_kernel(tc, a, b, out):
 
         for g, h in ((0, 0), (1, 0), (0, 1), (1, 1)):
             regroup(0, g, h, scopy)
-        for j in range(3):
+        for j in range(4):
             transpose_a(0, j)
         absolute(0)
         fold(0)
@@ -304,7 +330,6 @@ def tile_sparsebmm_t_kernel(tc, a, b, out):
         masked_copy(0, 0)
         fold_again(1)
         masked_copy(0, 1)
-        transpose_a(0, 3)
         indicate(1)
         quant_a(0, 0)
         quant_b(0, 0, 0)
@@ -318,36 +343,54 @@ def tile_sparsebmm_t_kernel(tc, a, b, out):
         make_mask(1)
         quant_b(0, 0, 1)
         absolute(2)
+        quant_b(0, 1, 1)
+        fold(2)
+        gate(1)
 
-        late = (0, 1, 1)
+        late = None
         for hf in range(NH):
             nb = hf // 2 + 1
             hb = hf % 2
             last = hf == NH - 1
-            quant_b(*late)
-            load_a(hf + 4)
+            if late is not None:
+                quant_b(*late)
+                gate(hf + 1)
+            if hf < NH - 2:
+                regroup_g(nb, 1, hb, SPLIT, 128, hf + 1)
+            load_a(hf + 5)
             if hb == 0:
                 load_b(nb + 1)
             if hf == 0:
                 products(0, ((0, 0, 0), (0, 1, 0)))
                 transpose_a(1, 0)
                 transpose_a(1, 1)
-                products(0, ((1, 0, 0),))
+                products(0, ((1, 0, 0), (1, 1, 0)))
+                transpose_a(1, 2)
+                transpose_a(1, 3)
             elif last:
                 products(hf, ((0, 0, 0), (0, 0, 1), (0, 1, 0)))
             else:
                 products(hf, ((0, 0, 0), (0, 1, 0), (0, 0, 1)))
             masked_copy(hf + 1, 0)
-            fold(hf + 2)
-            masked_copy(hf + 1, 1)
-            transpose_a(hf + 1, 2)
-            transpose_a(hf + 1, 3)
-            fold_again(hf + 2)
-            quant_a(hf + 1, 0)
-            indicate(hf + 2)
-            regroup(nb, 0, hb, scopy)
             if hf == 0:
-                products(0, ((1, 1, 0), (0, 0, 1), (0, 1, 1)))
+                fold_again(2)
+            masked_copy(hf + 1, 1)
+            if hf == 0:
+                indicate(2)
+                absolute(3)
+            masked_copy(hf + 1, 2)
+            masked_copy(hf + 1, 3)
+            count_rows(hf + 2)
+            transpose_a(hf + 2, 0)
+            transpose_a(hf + 2, 1)
+            counts_out(hf + 2)
+            regroup(nb, 0, hb, scopy)
+            fold(hf + 3)
+            quant_a(hf + 1, 0)
+            fold_again(hf + 3)
+            quant_a(hf + 1, 1)
+            if hf == 0:
+                products(0, ((0, 0, 1), (0, 1, 1)))
                 store(0, 0, 0, 2048)
             elif last:
                 products(hf, ((0, 1, 1),))
@@ -358,23 +401,18 @@ def tile_sparsebmm_t_kernel(tc, a, b, out):
                 products(hf, ((0, 1, 1),))
                 store(hf, 0, 0, 2048)
                 products(hf, ((1, 0, 0), (1, 1, 0)))
-            masked_copy(hf + 1, 2)
-            masked_copy(hf + 1, 3)
-            absolute(hf + 3)
-            count_rows(hf + 2)
-            transpose_a(hf + 2, 0)
-            regroup(nb, 1, hb, vcopy, 64, 128)
-            regroup(nb, 1, hb, scopy, 0, 64)
-            counts_out(hf + 2)
+            count_tiles(hf + 2)
+            transpose_a(hf + 2, 2)
+            transpose_a(hf + 2, 3)
+            make_mask(hf + 2)
+            indicate(hf + 3)
+            absolute(hf + 4)
+            regroup(nb, 1, hb, scopy, 0, SPLIT)
             if last:
                 products(hf, ((1, 1, 0), (1, 1, 1)))
                 store(hf, 1, 1024, 2048)
             else:
                 products(hf, ((1, 0, 1), (1, 1, 1)))
                 store(hf, 1, 0, 2048)
-            quant_a(hf + 1, 1)
-            count_tiles(hf + 2)
-            transpose_a(hf + 2, 1)
             quant_b(nb, 0, hb)
-            make_mask(hf + 2)
             late = (nb, 1, hb)

@@ -27,7 +27,7 @@ def tile_sparsebmm_t_kernel(tc, a, b, out):
     with ExitStack() as ctx:
         const = ctx.enter_context(tc.tile_pool(name="const", bufs=1))
         rawa = ctx.enter_context(tc.tile_pool(name="rawa", bufs=6))
-        rawb = ctx.enter_context(tc.tile_pool(name="rawb", bufs=2))
+        rawb = ctx.enter_context(tc.tile_pool(name="rawb", bufs=3))
         scr = ctx.enter_context(tc.tile_pool(name="scr", bufs=2))
         small = ctx.enter_context(tc.tile_pool(name="small", bufs=2))
         gap = ctx.enter_context(tc.tile_pool(name="gap", bufs=3))
@@ -85,6 +85,7 @@ def tile_sparsebmm_t_kernel(tc, a, b, out):
         load_a(2)
         load_b(1)
         load_a(3)
+        load_b(2)
         load_a(4)
 
         ident = const.tile([P, P], F32)
@@ -308,10 +309,9 @@ def tile_sparsebmm_t_kernel(tc, a, b, out):
         scopy = nc.scalar.copy
         vcopy = nc.vector.tensor_copy
 
-        def products(hf, group):
-            for c, j, h in group:
-                multiply(hf, c, j, h)
-                copy_out(hf, c, j, h, vcopy if hf == NH - 1 and h == 1 else scopy)
+        def product(hf, c, j, h, copy):
+            multiply(hf, c, j, h)
+            copy_out(hf, c, j, h, copy)
 
         for g, h in ((0, 0), (1, 0), (0, 1), (1, 1)):
             regroup(0, g, h, scopy)
@@ -330,89 +330,114 @@ def tile_sparsebmm_t_kernel(tc, a, b, out):
         masked_copy(0, 0)
         fold_again(1)
         masked_copy(0, 1)
-        indicate(1)
         quant_a(0, 0)
+        indicate(1)
         quant_b(0, 0, 0)
         quant_b(0, 1, 0)
         count_rows(1)
         masked_copy(0, 2)
         masked_copy(0, 3)
         counts_out(1)
+        product(0, 0, 0, 0, scopy)
+        product(0, 0, 1, 0, scopy)
         count_tiles(1)
+        transpose_a(1, 0)
+        transpose_a(1, 1)
+        absolute(2)
         quant_a(0, 1)
         make_mask(1)
         quant_b(0, 0, 1)
-        absolute(2)
-        quant_b(0, 1, 1)
+        product(0, 1, 0, 0, scopy)
+        product(0, 1, 1, 0, scopy)
+        transpose_a(1, 2)
+        transpose_a(1, 3)
         fold(2)
+        quant_b(0, 1, 1)
+        fold_again(2)
+        regroup(1, 0, 0, scopy)
+        absolute(3)
         gate(1)
 
-        late = None
-        for hf in range(NH):
-            nb = hf // 2 + 1
-            hb = hf % 2
-            last = hf == NH - 1
-            if late is not None:
-                quant_b(*late)
-                gate(hf + 1)
-            if hf < NH - 2:
-                regroup_g(nb, 1, hb, SPLIT, 128, hf + 1)
-            load_a(hf + 5)
-            if hb == 0:
-                load_b(nb + 1)
-            if hf == 0:
-                products(0, ((0, 0, 0), (0, 1, 0)))
-                transpose_a(1, 0)
-                transpose_a(1, 1)
-                products(0, ((1, 0, 0), (1, 1, 0)))
-                transpose_a(1, 2)
-                transpose_a(1, 3)
-            elif last:
-                products(hf, ((0, 0, 0), (0, 0, 1), (0, 1, 0)))
+        late = (1, 0, 0)
+        for hf in range(1, NH + 1):
+            odd = hf % 2 == 1
+            if odd:
+                first = ((hf + 1) // 2, 1, 0)
+                second = ((hf + 1) // 2, 0, 1)
             else:
-                products(hf, ((0, 0, 0), (0, 1, 0), (0, 0, 1)))
-            masked_copy(hf + 1, 0)
-            if hf == 0:
-                fold_again(2)
-            masked_copy(hf + 1, 1)
-            if hf == 0:
-                indicate(2)
-                absolute(3)
-            masked_copy(hf + 1, 2)
-            masked_copy(hf + 1, 3)
-            count_rows(hf + 2)
-            transpose_a(hf + 2, 0)
-            transpose_a(hf + 2, 1)
-            counts_out(hf + 2)
-            regroup(nb, 0, hb, scopy)
-            fold(hf + 3)
-            quant_a(hf + 1, 0)
-            fold_again(hf + 3)
-            quant_a(hf + 1, 1)
-            if hf == 0:
-                products(0, ((0, 0, 1), (0, 1, 1)))
+                first = (hf // 2, 1, 1)
+                second = (hf // 2 + 1, 0, 0)
+            end = hf == NH
+            tail = hf == NH - 1
+            if second[0] < NB:
+                regroup_g(*second, SPLIT, 128, hf)
+            load_a(hf + 4)
+            if odd:
+                load_b((hf + 1) // 2 + 2)
+            if hf == 1:
+                product(0, 0, 0, 1, scopy)
+                product(0, 0, 1, 1, scopy)
                 store(0, 0, 0, 2048)
-            elif last:
-                products(hf, ((0, 1, 1),))
-                store(hf, 0, 0, 2048)
-                products(hf, ((1, 0, 0), (1, 0, 1)))
-                store(hf, 1, 0, 1024)
+            elif end:
+                product(hf - 1, 1, 0, 0, scopy)
+                product(hf - 1, 1, 0, 1, vcopy)
+                store(hf - 1, 1, 0, 1024)
             else:
-                products(hf, ((0, 1, 1),))
-                store(hf, 0, 0, 2048)
-                products(hf, ((1, 0, 0), (1, 1, 0)))
-            count_tiles(hf + 2)
-            transpose_a(hf + 2, 2)
-            transpose_a(hf + 2, 3)
-            make_mask(hf + 2)
-            indicate(hf + 3)
-            absolute(hf + 4)
-            regroup(nb, 1, hb, scopy, 0, SPLIT)
-            if last:
-                products(hf, ((1, 1, 0), (1, 1, 1)))
-                store(hf, 1, 1024, 2048)
+                product(hf - 1, 1, 0, 0, scopy)
+                product(hf - 1, 1, 1, 0, scopy)
+            masked_copy(hf, 0)
+            if hf == 1:
+                indicate(2)
+            for j in range(1, 4):
+                masked_copy(hf, j)
+            if hf == 1:
+                count_rows(2)
+                counts_out(2)
             else:
-                products(hf, ((1, 0, 1), (1, 1, 1)))
-                store(hf, 1, 0, 2048)
-            quant_b(nb, 0, hb)
-            late = (nb, 1, hb)
+                counts_out(hf + 1)
+            if hf != NH - 2:
+                regroup(*first, scopy, 0, 64)
+            if hf == 1:
+                product(0, 1, 0, 1, scopy)
+                product(0, 1, 1, 1, scopy)
+                store(0, 1, 0, 2048)
+            elif end:
+                product(hf - 1, 1, 1, 0, scopy)
+                product(hf - 1, 1, 1, 1, vcopy)
+                store(hf - 1, 1, 1024, 2048)
+            else:
+                product(hf - 1, 1, 0, 1, scopy)
+                product(hf - 1, 1, 1, 1, scopy)
+                store(hf - 1, 1, 0, 2048)
+            if hf == NH - 2:
+                regroup(*first, vcopy)
+            fold(hf + 2)
+            quant_a(hf, 0)
+            fold_again(hf + 2)
+            quant_a(hf, 1)
+            transpose_a(hf + 1, 0)
+            transpose_a(hf + 1, 1)
+            count_tiles(hf + 1)
+            if hf != NH - 2:
+                regroup(*first, scopy, 64, 128)
+            make_mask(hf + 1)
+            indicate(hf + 2)
+            quant_b(*late)
+            if not odd:
+                quant_b(*first)
+            if not end:
+                product(hf, 0, 0, 0, scopy)
+                product(hf, 0, 1, 0, vcopy if tail else scopy)
+            transpose_a(hf + 1, 2)
+            transpose_a(hf + 1, 3)
+            regroup(*second, scopy, 0, SPLIT)
+            count_rows(hf + 2)
+            absolute(hf + 3)
+            if odd:
+                quant_b(*first)
+            if not end:
+                product(hf, 0, 0, 1, scopy)
+                product(hf, 0, 1, 1, vcopy if tail else scopy)
+                store(hf, 0, 0, 2048)
+            gate(hf + 1)
+            late = second

from contextlib import ExitStack

import concourse.mybir as mybir
from concourse.masks import make_identity

FLOPS = 2 * 4 * 1024 * 1024 * 1024

BF16 = mybir.dt.bfloat16
F32 = mybir.dt.float32
I32 = mybir.dt.int32
U32 = mybir.dt.uint32
U8 = mybir.dt.uint8
FP8X4 = mybir.dt.float8_e4m3fn_x4
ALU = mybir.AluOpType
AX = mybir.AxisListType

P = 128
NB = 4
NH = 2 * NB
THRESHOLD = 1e-6
HEAD_PIECES = 2
SPLIT = 56


def tile_sparsebmm_t_kernel(tc, a, b, out):
    nc = tc.nc
    with ExitStack() as ctx:
        const = ctx.enter_context(tc.tile_pool(name="const", bufs=1))
        rawa = ctx.enter_context(tc.tile_pool(name="rawa", bufs=6))
        rawb = ctx.enter_context(tc.tile_pool(name="rawb", bufs=3))
        scr = ctx.enter_context(tc.tile_pool(name="scr", bufs=2))
        small = ctx.enter_context(tc.tile_pool(name="small", bufs=2))
        gap = ctx.enter_context(tc.tile_pool(name="gap", bufs=3))
        gbp = ctx.enter_context(tc.tile_pool(name="gbp", bufs=4))
        codes = ctx.enter_context(tc.tile_pool(name="codes", bufs=2))
        outp = ctx.enter_context(tc.tile_pool(name="outp", bufs=4))
        ps_xt = ctx.enter_context(tc.psum_pool(name="ps_xt", bufs=4))
        ps_acc = ctx.enter_context(tc.psum_pool(name="ps_acc", bufs=3))
        ps_cnt = ctx.enter_context(tc.psum_pool(name="ps_cnt", bufs=1))


        ctx.enter_context(tc.manual_schedule())
        a_raw = {}
        b_raw = {}

        def load_a(hf):
            if hf >= NH:
                return
            a_t = rawa.tile([P, 4096], BF16, tag="a_raw", name="a_raw%d" % hf)
            a_raw[hf] = a_t
            view = a[hf // 2][512 * (hf % 2):512 * (hf % 2) + 512, :].rearrange("(p j) k -> p (j k)", j=4)
            pieces = HEAD_PIECES if hf == 0 else 1
            w = 4096 // pieces
            for c in range(pieces):
                nc.sync.dma_start(out=a_t[:, w * c:w * (c + 1)], in_=view[:, w * c:w * (c + 1)])

        def new_b(i):
            b_t = rawb.tile([P, 8192], BF16, tag="b_raw", name="b_raw%d" % i)
            b_raw[i] = b_t

        def load_b(i):
            if i >= NB:
                return
            new_b(i)
            for g in range(2):
                nc.sync.dma_start(
                    out=b_raw[i][:, 4096 * g:4096 * (g + 1)],
                    in_=b[i][512 * g:512 * (g + 1), :].rearrange("(q t) n -> q (t n)", t=4),
                )

        def load_b_quarter(g, h):
            lo = 4096 * g + 2048 * h
            nc.sync.dma_start(
                out=b_raw[0][:, lo:lo + 2048].rearrange("q (t n) -> q t n", t=4),
                in_=b[0][512 * g:512 * (g + 1), 512 * h:512 * (h + 1)].rearrange("(q t) n -> q t n", t=4),
            )

        new_b(0)
        load_a(0)
        load_b_quarter(0, 0)
        load_a(1)
        load_b_quarter(1, 0)
        load_b_quarter(0, 1)
        load_b_quarter(1, 1)
        load_a(2)
        load_b(1)
        load_a(3)
        load_b(2)
        load_a(4)

        ident = const.tile([P, P], F32)
        make_identity(nc, ident[:])
        rows8 = const.tile([P, 8], F32)
        nc.vector.tensor_reduce(out=rows8[:], in_=ident[:].rearrange("p (g c) -> p g c", c=16), axis=AX.X, op=ALU.add)
        rowsel = const.tile([P, 8], BF16)
        nc.scalar.copy(out=rowsel[:], in_=rows8[:])
        halves = const.tile([P, 2], F32)
        nc.vector.tensor_reduce(out=halves[:], in_=ident[:].rearrange("p (g c) -> p g c", c=64), axis=AX.X, op=ALU.add)
        ksel = const.tile([P, 512], BF16)
        nc.vector.memset(ksel[:].bitcast(I32), 0)
        for w in range(4):
            nc.vector.tensor_copy(
                out=ksel[:, 128 * w + 32 * w:128 * w + 32 * w + 32].rearrange("p (h c) -> p h c", c=16),
                in_=halves[:].unsqueeze(2).to_broadcast([P, 2, 16]),
            )


        state = {}

        def absolute(hf):
            if hf >= NH:
                return
            ab = scr.tile([P, 4096], BF16, tag="ab", name="ab_%d" % hf)
            state["ab", hf] = ab
            pieces = HEAD_PIECES if hf == 0 else 1
            w = 4096 // pieces
            for c in range(pieces):
                nc.vector.tensor_scalar(
                    out=ab[:, w * c:w * (c + 1)].bitcast(I32),
                    in0=a_raw[hf][:, w * c:w * (c + 1)].bitcast(I32),
                    scalar1=0x7FFF7FFF, scalar2=None, op0=ALU.bitwise_and,
                )

        def fold(hf):
            if hf >= NH:
                return
            ab = state["ab", hf]
            mx = scr.tile([P, 2048], BF16, tag="mx", name="mx_%d" % hf)
            state["mx", hf] = mx
            nc.vector.tensor_tensor(out=mx[:], in0=ab[:, 0:2048], in1=ab[:, 2048:4096], op=ALU.max)

        def fold_again(hf):
            if hf >= NH:
                return
            mx = state["mx", hf]
            mx2 = scr.tile([P, 1024], BF16, tag="mx2", name="mx2_%d" % hf)
            state["mx2", hf] = mx2
            nc.vector.tensor_tensor(out=mx2[:], in0=mx[:, 0:1024], in1=mx[:, 1024:2048], op=ALU.max)

        def indicate(hf):
            if hf >= NH:
                return
            ind = scr.tile([P, 1024], BF16, tag="ind", name="ind_%d" % hf)
            state["ind", hf] = ind
            nc.vector.tensor_scalar(
                out=ind[:], in0=state["mx2", hf][:], scalar1=THRESHOLD, scalar2=None, op0=ALU.is_gt)

        def count_rows(hf):
            if hf >= NH:
                return
            cnt = ps_cnt.tile([P, 80], F32, tag="cnt", name="cnt_%d" % hf)
            state["cnt", hf] = cnt
            ind = state["ind", hf]
            for w in range(8):
                nc.tensor.matmul(
                    out=cnt[:, 8 * w:8 * w + 8], lhsT=ind[:, 128 * w:128 * w + 128], rhs=rowsel[:],
                    start=True, stop=True,
                )

        def counts_out(hf):
            if hf >= NH:
                return
            c1 = small.tile([P, 64], BF16, tag="c1", name="c1_%d" % hf)
            state["c1", hf] = c1
            nc.vector.tensor_copy(out=c1[:], in_=state["cnt", hf][:, 0:64])

        def count_tiles(hf):
            if hf >= NH:
                return
            c1 = state["c1", hf]
            for w in range(4):
                nc.tensor.matmul(
                    out=state["cnt", hf][:, 64:80], lhsT=ksel[:, 128 * w:128 * (w + 1)],
                    rhs=c1[:].rearrange("p (g w r) -> p g w r", g=2, w=4)[:, :, w, :],
                    start=(w == 0), stop=(w == 3),
                )

        def make_mask(hf):
            if hf >= NH:
                return
            mask = small.tile([P, 32], BF16, tag="mask", name="mask_%d" % hf)
            state["mask", hf] = mask
            nc.vector.tensor_scalar(
                out=mask[:].rearrange("p (c e) -> p c e", e=2),
                in0=state["cnt", hf][:, 64:80].unsqueeze(2).to_broadcast([P, 16, 2]),
                scalar1=1.0, scalar2=None, op0=ALU.min,
            )

        def gate(hf):
            if hf >= NH:
                return
            one = small.tile([P, 1], F32, tag="one", name="one_%d" % hf)
            state["one", hf] = one
            nc.vector.tensor_scalar(
                out=one[:], in0=state["mask", hf][:, 0:1], scalar1=0.0, scalar2=1.0, op0=ALU.mult, op1=ALU.add
            )

        def transpose_a(hf, j):
            if hf >= NH:
                return
            aw = a_raw[hf][:].bitcast(F32)
            xt = ps_xt.tile([P, 512], F32, tag="xt", name="xt_%d_%d" % (hf, j))
            state["xt", hf, j] = xt
            for g in range(2):
                for u in range(2):
                    w0 = 512 * j + 256 * g + u
                    nc.tensor.transpose(
                        xt[:, 256 * u + 128 * g:256 * u + 128 * (g + 1)], aw[:, w0:w0 + 255:2], ident[:]
                    )

        def masked_copy(hf, j):
            if hf >= NH:
                return
            if j % 2 == 0:
                ga = gap.tile([P, 2048], BF16, tag="ga", name="ga_%d_%d" % (hf, j // 2), align_bytes=64)
                state["ga", hf, j // 2] = ga
            nc.vector.tensor_tensor(
                out=state["ga", hf, j // 2][:, 1024 * (j % 2):1024 * (j % 2 + 1)],
                in0=state["xt", hf, j][:].bitcast(BF16).rearrange("q (u m e) -> q m u e", u=2, e=2),
                in1=state["mask", hf][:].rearrange("q (r e) -> q r e", e=2).unsqueeze(2).to_broadcast([P, 16, 32, 2]),
                op=ALU.mult,
            )

        def quant_a(hf, c):
            if hf >= NH:
                return
            if c == 0:
                state["ac", hf] = codes.tile([P, 1024], U32, tag="ac", name="ac_%d" % hf, align_bytes=64)
                state["asc", hf] = codes.tile([P, 1024], U8, tag="asc", name="asc_%d" % hf, align_bytes=64)
            nc.vector.quantize_mx(
                out=state["ac", hf][:, 512 * c:512 * (c + 1)].bitcast(FP8X4),
                scales=state["asc", hf][:, 512 * c:512 * (c + 1)],
                in_=state["ga", hf, c][:],
            )

        def regroup(i, g, h, copy, lo4=0, hi4=128):
            if i >= NB:
                return
            if ("gb", i, g, h) not in state:
                state["gb", i, g, h] = gbp.tile(
                    [P, 2048], BF16, tag="gb", name="gb_%d_%d_%d" % (i, g, h), align_bytes=64)
            gb = state["gb", i, g, h]
            if i == 0:
                lo = 4096 * g + 2048 * h
                src = b_raw[0][:, lo:lo + 2048].rearrange("q (t n) -> q t n", t=4)
            else:
                src = b_raw[i][:, 4096 * g:4096 * (g + 1)].rearrange(
                    "q (t n) -> q t n", t=4)[:, :, 512 * h:512 * (h + 1)]
            copy(
                out=gb[:].rearrange("q (c i t) -> q c t i", i=4, t=4)[:, lo4:hi4],
                in_=src.rearrange("q t (c i) -> q c t i", i=4)[:, lo4:hi4],
            )

        def regroup_g(i, g, h, lo4, hi4, hf):
            if i >= NB:
                return
            if ("gb", i, g, h) not in state:
                state["gb", i, g, h] = gbp.tile(
                    [P, 2048], BF16, tag="gb", name="gb_%d_%d_%d" % (i, g, h), align_bytes=64)
            gb = state["gb", i, g, h]
            src = b_raw[i][:, 4096 * g:4096 * (g + 1)].rearrange(
                "q (t n) -> q t n", t=4)[:, :, 512 * h:512 * (h + 1)]
            nc.gpsimd.tensor_scalar(
                out=gb[:].rearrange("q (n t) -> q n t", t=4)[:, 4 * lo4:4 * hi4],
                in0=src.rearrange("q t n -> q n t")[:, 4 * lo4:4 * hi4],
                scalar1=state["one", hf][:], scalar2=0.0, op0=ALU.mult, op1=ALU.add,
            )

        def quant_b(i, g, h):
            if i >= NB:
                return
            if (g, h) == (0, 0):
                state["bc", i] = codes.tile([P, 2048], U32, tag="bc", name="bc_%d" % i, align_bytes=64)
                state["bsc", i] = codes.tile([P, 2048], U8, tag="bsc", name="bsc_%d" % i, align_bytes=64)
            lo = 1024 * g + 512 * h
            nc.vector.quantize_mx(
                out=state["bc", i][:, lo:lo + 512].bitcast(FP8X4),
                scales=state["bsc", i][:, lo:lo + 512],
                in_=state["gb", i, g, h][:],
            )

        def multiply(hf, c, j, h):
            i = hf // 2
            acc = ps_acc.tile([P, 512], F32, tag="acc", name="acc_%d_%d_%d_%d" % (hf, c, j, h))
            state["acc", hf, c, j, h] = acc
            for g in range(2):
                lo = 512 * c + 256 * j + 128 * g
                ro = 1024 * g + 512 * h
                nc.tensor.matmul_mx(
                    out=acc[:],
                    lhsT=state["ac", hf][:, lo:lo + 128].bitcast(FP8X4),
                    lhsT_scale=state["asc", hf][:, lo:lo + 128],
                    rhs=state["bc", i][:, ro:ro + 512].bitcast(FP8X4),
                    rhs_scale=state["bsc", i][:, ro:ro + 512],
                    start=(g == 0),
                    stop=(g == 1),
                )

        def copy_out(hf, c, j, h, copy):
            if ("o", hf, c) not in state:
                state["o", hf, c] = outp.tile([P, 2048], F32, tag="o", name="o_%d_%d" % (hf, c))
            oo = 1024 * j + 512 * h
            copy(out=state["o", hf, c][:, oo:oo + 512], in_=state["acc", hf, c, j, h][:])

        def store(hf, c, lo, hi):
            dst = out[hf // 2][512 * (hf % 2):512 * (hf % 2) + 512, :].rearrange("(p j) n -> p (j n)", j=4)
            nc.sync.dma_start(out=dst[:, 2048 * c + lo:2048 * c + hi], in_=state["o", hf, c][:, lo:hi])

        scopy = nc.scalar.copy
        vcopy = nc.vector.tensor_copy

        def product(hf, c, j, h, copy):
            multiply(hf, c, j, h)
            copy_out(hf, c, j, h, copy)

        for g, h in ((0, 0), (1, 0), (0, 1), (1, 1)):
            regroup(0, g, h, scopy)
        for j in range(4):
            transpose_a(0, j)
        absolute(0)
        fold(0)
        fold_again(0)
        indicate(0)
        count_rows(0)
        absolute(1)
        counts_out(0)
        count_tiles(0)
        fold(1)
        make_mask(0)
        masked_copy(0, 0)
        fold_again(1)
        masked_copy(0, 1)
        quant_a(0, 0)
        indicate(1)
        quant_b(0, 0, 0)
        quant_b(0, 1, 0)
        count_rows(1)
        masked_copy(0, 2)
        masked_copy(0, 3)
        counts_out(1)
        product(0, 0, 0, 0, scopy)
        product(0, 0, 1, 0, scopy)
        count_tiles(1)
        transpose_a(1, 0)
        transpose_a(1, 1)
        absolute(2)
        quant_a(0, 1)
        make_mask(1)
        quant_b(0, 0, 1)
        product(0, 1, 0, 0, scopy)
        product(0, 1, 1, 0, scopy)
        transpose_a(1, 2)
        transpose_a(1, 3)
        fold(2)
        quant_b(0, 1, 1)
        fold_again(2)
        regroup(1, 0, 0, scopy)
        absolute(3)
        gate(1)

        late = (1, 0, 0)
        for hf in range(1, NH + 1):
            odd = hf % 2 == 1
            if odd:
                first = ((hf + 1) // 2, 1, 0)
                second = ((hf + 1) // 2, 0, 1)
            else:
                first = (hf // 2, 1, 1)
                second = (hf // 2 + 1, 0, 0)
            end = hf == NH
            tail = hf == NH - 1
            if second[0] < NB:
                regroup_g(*second, SPLIT, 128, hf)
            load_a(hf + 4)
            if odd:
                load_b((hf + 1) // 2 + 2)
            if hf == 1:
                product(0, 0, 0, 1, scopy)
                product(0, 0, 1, 1, scopy)
                store(0, 0, 0, 2048)
            elif end:
                product(hf - 1, 1, 0, 0, scopy)
                product(hf - 1, 1, 0, 1, vcopy)
                store(hf - 1, 1, 0, 1024)
            else:
                product(hf - 1, 1, 0, 0, scopy)
                product(hf - 1, 1, 1, 0, scopy)
            masked_copy(hf, 0)
            if hf == 1:
                indicate(2)
            for j in range(1, 4):
                masked_copy(hf, j)
            if hf == 1:
                count_rows(2)
                counts_out(2)
            else:
                counts_out(hf + 1)
            if hf != NH - 2:
                regroup(*first, scopy, 0, 64)
            if hf == 1:
                product(0, 1, 0, 1, scopy)
                product(0, 1, 1, 1, scopy)
                store(0, 1, 0, 2048)
            elif end:
                product(hf - 1, 1, 1, 0, scopy)
                product(hf - 1, 1, 1, 1, vcopy)
                store(hf - 1, 1, 1024, 2048)
            else:
                product(hf - 1, 1, 0, 1, scopy)
                product(hf - 1, 1, 1, 1, scopy)
                store(hf - 1, 1, 0, 2048)
            if hf == NH - 2:
                regroup(*first, vcopy)
            fold(hf + 2)
            quant_a(hf, 0)
            fold_again(hf + 2)
            quant_a(hf, 1)
            transpose_a(hf + 1, 0)
            transpose_a(hf + 1, 1)
            count_tiles(hf + 1)
            if hf != NH - 2:
                regroup(*first, scopy, 64, 128)
            make_mask(hf + 1)
            indicate(hf + 2)
            quant_b(*late)
            if not odd:
                quant_b(*first)
            if not end:
                product(hf, 0, 0, 0, scopy)
                product(hf, 0, 1, 0, vcopy if tail else scopy)
            transpose_a(hf + 1, 2)
            transpose_a(hf + 1, 3)
            regroup(*second, scopy, 0, SPLIT)
            count_rows(hf + 2)
            absolute(hf + 3)
            if odd:
                quant_b(*first)
            if not end:
                product(hf, 0, 0, 1, scopy)
                product(hf, 0, 1, 1, vcopy if tail else scopy)
                store(hf, 0, 0, 2048)
            gate(hf + 1)
            late = second
